import numpy as np
import ml_dtypes


def mxq(x, axis, fmt="e4m3"):
    dtype, down = {"e4m3": (ml_dtypes.float8_e4m3fn, 7), "e5m2": (ml_dtypes.float8_e5m2, 14)}[fmt]
    v = np.moveaxis(np.asarray(x, np.float32).astype(ml_dtypes.bfloat16).astype(np.float64), axis, -1)
    blocks = v.reshape(v.shape[:-1] + (-1, 32))
    amax = np.abs(blocks).max(-1, keepdims=True)
    byte = np.maximum(np.where(amax > 0, np.frexp(amax)[1] - 1 + 127, 0) - down, 1)
    scale = np.exp2(byte - 127.0)
    codes = (blocks / scale).astype(np.float32).astype(dtype).astype(np.float64)
    return np.moveaxis((codes * scale).reshape(v.shape), -1, axis)


WIDE = False


def mx_kscale(k):
    if not WIDE:
        return np.ones(k)
    levels = np.array([10, -10, 5, -5, 0])
    if k % 512:
        return np.exp2(np.random.permutation(np.resize(levels, k // 32))).repeat(32)
    a = np.empty((k // 512, 16))
    for p in range(k // 512):
        a[p, :8] = np.random.permutation(np.resize(levels, 8))
        for g in range(8):
            far = levels[np.abs(levels - a[p, g]) >= 10]
            a[p, g + 8] = far[np.random.randint(len(far))]
    return np.exp2(a.ravel()).repeat(32)


BF16 = ml_dtypes.bfloat16


def bf(x):
    return np.asarray(x, np.float32).astype(BF16)


def f64(x):
    return np.asarray(x).astype(np.float64)


E2M1 = np.array([0.0, 0.5, 1.0, 1.5, 2.0, 3.0, 4.0, 6.0, -0.0, -0.5, -1.0, -1.5, -2.0, -3.0, -4.0, -6.0])


def pack_weight(w, fmt):
    k, n = w.shape
    w = f64(bf(w)).reshape(k // 32, 32, n)
    amax = np.abs(w).max(1)
    if fmt == "e4m3":
        byte = np.frexp(amax)[1] - 1 + 127 - 7
    else:
        mant, ex = np.frexp(amax / 6.0)
        byte = np.where(mant > 0.5, ex, ex - 1) + 127
    byte = np.clip(np.where(amax > 0, byte, 1), 1, 254)
    scaled = (w * np.exp2(127.0 - byte)[:, None, :]).reshape(k, n).astype(np.float32)
    by_word = np.ascontiguousarray(scaled.reshape(k // 512, 128, 4, n).transpose(0, 1, 3, 2))
    if fmt == "e4m3":
        words = by_word.astype(ml_dtypes.float8_e4m3fn).view(np.uint8)
    else:
        c = by_word.astype(ml_dtypes.float4_e2m1fn).view(np.uint8) & 0xF
        words = c[..., 0::2] | (c[..., 1::2] << 4)
    return np.ascontiguousarray(words), np.ascontiguousarray(byte.astype(np.uint8).reshape(k // 512, 16, n))


def unpack_weight(words, scales, fmt):
    g, p, n, _ = words.shape
    if fmt == "e4m3":
        vals = np.ascontiguousarray(words).view(ml_dtypes.float8_e4m3fn).astype(np.float64)
    else:
        nib = np.empty((g, p, n, 4), np.uint8)
        nib[..., 0::2] = words & 0xF
        nib[..., 1::2] = words >> 4
        vals = E2M1[nib]
    vals = vals * np.repeat(np.exp2(scales.astype(np.float64) - 127.0), 8, axis=1)[..., None]
    return vals.transpose(0, 1, 3, 2).reshape(g * 512, n)


B, T, D, H = 4, 256, 512, 2048
N = B * T
EMA0 = 1.0


def sigmoid(v):
    return 1.0 / (1.0 + np.exp(-v))


def surprise_gate(err):
    err_mag = np.sqrt(np.sum(err * err)) / N
    ema = 0.95 * EMA0 + 0.05 * err_mag
    return np.minimum(err_mag / np.maximum(ema, 1e-8), 3.0)


def draw0():
    s, t = mx_kscale(D), mx_kscale(N)
    err = bf(np.random.standard_normal((N, D)) * 2.3 * s[None, :] * t[:, None])
    words, scales = pack_weight(np.random.standard_normal((D, H)) / np.sqrt(D) / s[:, None], "e4m3")
    return {"err": err,
            "W_down_words": words,
            "W_down_scales": scales,
            "gate_pre": bf(np.random.standard_normal((N, H))),
            "up_pre": bf(np.random.standard_normal((N, H))),
            "x_pred": bf(np.random.standard_normal((N, D)) / t[:, None])}


def core(err, W_down_words, W_down_scales, gate_pre, up_pre, x_pred):
    err, gate_pre, up_pre = f64(err), f64(gate_pre), f64(up_pre)
    sg = surprise_gate(err)
    d_h = mxq(err, 1, "e4m3") @ unpack_weight(W_down_words, W_down_scales, "e4m3")
    sig = sigmoid(gate_pre)
    gate_act = gate_pre * sig
    d_gate_act = d_h * up_pre
    d_up_val = d_h * gate_act
    d_gate_pre = d_gate_act * sig * (1.0 + gate_pre * (1.0 - sig))
    xq = mxq(f64(x_pred), 0, "e4m3")
    grad_gate = (mxq(d_gate_pre, 0, "e4m3").T @ xq) / N
    grad_up = (mxq(d_up_val, 0, "e4m3").T @ xq) / N
    return grad_up * sg, grad_gate * sg


def e4m3fn_bytes(y):
    return np.clip(np.asarray(y, np.float64), -448.0, 448.0).astype(np.float32).astype(ml_dtypes.float8_e4m3fn).view(np.uint8)


def e4m3fn_values(b):
    return np.asarray(b, np.uint8).view(ml_dtypes.float8_e4m3fn).astype(np.float64)


def setup_inputs():
    d = draw0()
    x0 = np.asarray(d['x_pred']).astype(np.float64)
    s = (np.max(np.abs(x0), axis=(1,), keepdims=True) / 448.0).astype(np.float32)
    out = {}
    for k, v in d.items():
        if k == 'x_pred':
            out['x_pred_bytes'] = e4m3fn_bytes(x0 / s.astype(np.float64))
            out['x_pred_scale'] = s
        else:
            out[k] = v
    return out


def reference(err, W_down_words, W_down_scales, gate_pre, up_pre, x_pred_bytes, x_pred_scale):
    return core(err, W_down_words, W_down_scales, gate_pre, up_pre, e4m3fn_values(x_pred_bytes) * x_pred_scale.astype(np.float64))

@@ -1,0 +1,338 @@
+from contextlib import ExitStack
+
+import concourse.mybir as mybir
+from concourse.masks import make_identity
+
+TOKENS, D, H = 1024, 512, 2048
+FLOPS = 3 * 2 * TOKENS * D * H
+
+F32 = mybir.dt.float32
+BF16 = mybir.dt.bfloat16
+I32 = mybir.dt.int32
+U32 = mybir.dt.uint32
+U8 = mybir.dt.uint8
+FP8 = mybir.dt.float8_e4m3fn
+FP8X4 = mybir.dt.float8_e4m3fn_x4
+ALU = mybir.AluOpType
+ACT = mybir.ActivationFunctionType
+
+P = 128
+PACK = 4
+GROUP = P * PACK
+GROUPS = TOKENS // GROUP
+UNIT = 128
+UNITS = H // UNIT
+CHUNKS = (256, 256, 512, 512, 512)
+W_CHUNKS = (256, 768, 1024)
+
+
+def starts_of(widths):
+    starts = []
+    for w in widths:
+        starts.append(sum(widths[: len(starts)]))
+    return starts
+
+
+def locate(starts, widths, h0):
+    for c, (s, w) in enumerate(zip(starts, widths)):
+        if s <= h0 < s + w:
+            return c, h0 - s
+    raise ValueError("h0 out of range")
+
+
+def tile_continuummemorysystem_pa_w8_kernel(
+    tc, err, w_words, w_scales, gate_pre, up_pre, x_bytes, x_scale, out_0, out_1
+):
+    nc = tc.nc
+    chunk_starts = starts_of(CHUNKS)
+    w_starts = starts_of(W_CHUNKS)
+
+    with ExitStack() as ctx:
+        keep = ctx.enter_context(tc.tile_pool(name="keep", bufs=1))
+        acts = ctx.enter_context(tc.tile_pool(name="acts", bufs=3))
+        work = ctx.enter_context(tc.tile_pool(name="work", bufs=2))
+        results = ctx.enter_context(tc.tile_pool(name="results", bufs=5))
+        dh_pool = ctx.enter_context(tc.psum_pool(name="dh_pool", bufs=3))
+        u_pool = ctx.enter_context(tc.psum_pool(name="u_pool", bufs=2))
+        out_pool = ctx.enter_context(tc.psum_pool(name="out_pool", bufs=3))
+        ctx.enter_context(tc.manual_schedule())
+
+        one_col = keep.tile([P, 1], F32)
+        half = keep.tile([P, 1], F32)
+        ones = keep.tile([P, P], F32)
+        planes = keep.tile([P, H], U8, align_bytes=64)
+        silu_warm = keep.tile([P, 1], F32)
+        nc.vector.memset(one_col[:], 1.0)
+        nc.vector.memset(planes[:].bitcast(I32), 0)
+        nc.vector.memset(half[:], 0.5)
+        nc.vector.memset(ones[:], 1.0)
+        nc.scalar.activation(out=silu_warm[:], in_=one_col[:], func=ACT.Silu)
+        ident_f32 = keep.tile([P, P], F32)
+        ident_bf = keep.tile([P, P], BF16)
+        make_identity(nc, ident_f32[:])
+        make_identity(nc, ident_bf[:])
+
+        x_raw = keep.tile([P, GROUPS * PACK, D], U8, align_bytes=64)
+        xs = keep.tile([P, GROUPS * PACK], F32)
+        x_view = x_bytes.rearrange("(g p t) n -> g p t n", p=P, t=PACK)
+        for g in range(GROUPS):
+            nc.sync.dma_start(out=x_raw[:, PACK * g : PACK * (g + 1), :], in_=x_view[g])
+        nc.sync.dma_start(
+            out=xs[:].rearrange("p (g t) -> p g t", t=PACK), in_=x_scale.rearrange("(g p t) o -> p g (t o)", p=P, t=PACK)
+        )
+
+        err_view = err.rearrange("(g p t) k -> g p t k", p=P, t=PACK)
+        err_raw = []
+        for g in range(GROUPS):
+            e = keep.tile([P, PACK, D], BF16, name=f"err_raw{g}")
+            nc.sync.dma_start(out=e[:], in_=err_view[g])
+            err_raw.append(e)
+
+        for q in range(4):
+            nc.sync.dma_start(
+                out=planes[32 * q : 32 * q + 4, :].bitcast(I32),
+                in_=w_scales[0, 4 * q : 4 * q + 4, :].bitcast(I32),
+            )
+
+        w_flat = w_words[0].rearrange("p n t -> p (n t)")
+        w_tiles = [keep.tile([P, w], U32, align_bytes=64, name=f"w{c}") for c, w in enumerate(W_CHUNKS)]
+
+        def load_w(c):
+            a, w = w_starts[c], W_CHUNKS[c]
+            nc.sync.dma_start(
+                out=w_tiles[c][:].bitcast(I32), in_=w_flat[:, PACK * a : PACK * (a + w)].bitcast(I32)
+            )
+
+        gate_view = gate_pre.rearrange("(g p t) h -> g p t h", p=P, t=PACK)
+        up_view = up_pre.rearrange("(g p t) h -> g p t h", p=P, t=PACK)
+        gate_tiles = [keep.tile([P, GROUPS * PACK, w], BF16, name=f"gate{c}") for c, w in enumerate(CHUNKS)]
+        up_tiles = [keep.tile([P, GROUPS * PACK, w], BF16, name=f"up{c}") for c, w in enumerate(CHUNKS)]
+
+        def load_h(view, tiles, c):
+            a, w = chunk_starts[c], CHUNKS[c]
+            for g in range(GROUPS):
+                nc.sync.dma_start(
+                    out=tiles[c][:, PACK * g : PACK * (g + 1), :], in_=view[g][:, :, a : a + w]
+                )
+
+        load_w(0)
+        load_h(gate_view, gate_tiles, 0)
+        load_h(up_view, up_tiles, 0)
+        load_h(gate_view, gate_tiles, 1)
+        load_h(up_view, up_tiles, 1)
+        load_w(1)
+        for c in range(2, len(CHUNKS)):
+            load_h(gate_view, gate_tiles, c)
+            load_h(up_view, up_tiles, c)
+            if c == 2:
+                load_w(2)
+
+        x_wide = keep.tile([P, GROUPS * PACK, D], BF16)
+        x_grouped = keep.tile([P, GROUPS, D, PACK], BF16, align_bytes=64)
+        for j in range(GROUPS * PACK):
+            nc.vector.tensor_scalar(
+                out=x_wide[:, j, :], in0=x_raw[:, j, :].bitcast(FP8), scalar1=xs[:, j : j + 1], scalar2=None, op0=ALU.mult
+            )
+        for g in range(GROUPS):
+            nc.vector.tensor_copy(
+                out=x_grouped[:, g].rearrange("p (c i) t -> p c t i", i=4),
+                in_=x_wide[:, PACK * g : PACK * (g + 1), :].rearrange("p t (c i) -> p c t i", i=4),
+            )
+
+        err_grouped = [keep.tile([P, PACK, P, PACK], BF16, align_bytes=64, name=f"err_grouped{g}") for g in range(GROUPS)]
+        err_codes = keep.tile([P, GROUPS, PACK * P], U32, align_bytes=64)
+        err_scales = keep.tile([P, GROUPS, PACK * P], U8, align_bytes=64)
+        x_codes = keep.tile([P, GROUPS, D], U32, align_bytes=64)
+        x_scales = keep.tile([P, GROUPS, D], U8, align_bytes=64)
+        for g in range(GROUPS):
+            for pair in range(2):
+                bank = out_pool.tile([P, 2, 2, P], F32, tag="out")
+                for s in range(2):
+                    words = err_raw[g][:, 2 * pair + s, :].bitcast(F32)
+                    for u in range(2):
+                        nc.tensor.transpose(bank[:, s, u, :], words[:, u : D // 2 : 2], ident_f32[:])
+                nc.scalar.copy(
+                    out=err_grouped[g][:, 2 * pair : 2 * pair + 2].rearrange("p s r e -> p s (r e)").bitcast(F32).rearrange(
+                        "p s (r u) -> p s r u", u=2
+                    ),
+                    in_=bank[:].rearrange("p s u r -> p s r u"),
+                )
+            nc.vector.quantize_mx(
+                out=err_codes[:, g, :].bitcast(FP8X4),
+                scales=err_scales[:, g, :],
+                in_=err_grouped[g][:].rearrange("p t r e -> p (t r e)"),
+            )
+            nc.vector.quantize_mx(
+                out=x_codes[:, g, :].bitcast(FP8X4),
+                scales=x_scales[:, g, :],
+                in_=x_grouped[:, g].rearrange("p n t -> p (n t)"),
+            )
+
+        th, sl, dh, uu, p2, yy, dup, dgate, codes = {}, {}, {}, {}, {}, {}, {}, {}, {}
+
+        def column_block(tiles, i):
+            c, off = locate(chunk_starts, CHUNKS, UNIT * i)
+            return tiles[c][:, :, off : off + UNIT]
+
+        def gate_activations(i):
+            g_view = column_block(gate_tiles, i).rearrange("p (g t) n -> p g n t", t=PACK)
+            th[i] = acts.tile([P, GROUPS, UNIT, PACK], F32, name="th")
+            sl[i] = acts.tile([P, GROUPS, UNIT, PACK], F32, name="sl")
+            nc.scalar.activation(out=th[i][:], in_=g_view, func=ACT.Tanh, scale=0.5)
+            nc.scalar.activation(out=sl[i][:], in_=g_view, func=ACT.Silu, scale=-1.0)
+
+        def first_matmuls(i):
+            c, off = locate(w_starts, W_CHUNKS, UNIT * i)
+            for g in range(GROUPS):
+                bank = dh_pool.tile([P, PACK, UNIT], F32, tag="dh")
+                for t in range(PACK):
+                    nc.tensor.matmul_mx(
+                        out=bank[:, t, :],
+                        lhsT=err_codes[:, g, P * t : P * (t + 1)].bitcast(FP8X4),
+                        lhsT_scale=err_scales[:, g, P * t : P * (t + 1)],
+                        rhs=w_tiles[c][:, off : off + UNIT].bitcast(FP8X4),
+                        rhs_scale=planes[:, UNIT * i : UNIT * (i + 1)],
+                        start=True,
+                        stop=True,
+                    )
+                dh[i, g] = bank
+            for g in range(GROUPS):
+                bank = u_pool.tile([P, PACK, UNIT], F32, tag="uu")
+                nc.tensor.matmul(
+                    bank[:], ident_bf[:], column_block(up_tiles, i)[:, PACK * g : PACK * (g + 1), :], start=True, stop=True
+                )
+                uu[i, g] = bank
+
+        def psum_products(i):
+            p2[i] = work.tile([P, GROUPS, UNIT * PACK], F32, name="p2")
+            yy[i] = work.tile([P, GROUPS, UNIT * PACK], F32, name="yy")
+            for g in range(GROUPS):
+                nc.vector.scalar_tensor_tensor(
+                    out=p2[i][:, g].rearrange("p (n t) -> p n t", t=PACK),
+                    in0=th[i][:, g],
+                    scalar=1.0,
+                    in1=dh[i, g][:].rearrange("p t n -> p n t"),
+                    op0=ALU.add,
+                    op1=ALU.mult,
+                )
+            for g in range(GROUPS):
+                nc.vector.scalar_tensor_tensor(
+                    out=yy[i][:, g].rearrange("p (n t) -> p n t", t=PACK),
+                    in0=sl[i][:, g],
+                    scalar=-1.0,
+                    in1=uu[i, g][:].rearrange("p t n -> p n t"),
+                    op0=ALU.add,
+                    op1=ALU.mult,
+                )
+
+        def up_product(i):
+            dup[i] = work.tile([P, GROUPS, UNIT * PACK], BF16, name="dup", align_bytes=64)
+            g_view = column_block(gate_tiles, i).rearrange("p (g t) n -> p g n t", t=PACK)
+            for g in range(GROUPS):
+                nc.gpsimd.tensor_tensor(
+                    out=dup[i][:, g].rearrange("p (n t) -> p n t", t=PACK),
+                    in0=p2[i][:, g].rearrange("p (n t) -> p n t", t=PACK),
+                    in1=g_view[:, g],
+                    op=ALU.mult,
+                )
+
+        def gate_product(i):
+            dgate[i] = work.tile([P, GROUPS, UNIT * PACK], BF16, name="dgate", align_bytes=64)
+            nc.vector.tensor_tensor(out=dgate[i][:], in0=p2[i][:], in1=yy[i][:], op=ALU.mult)
+
+        def quantize(i):
+            c_gate = work.tile([P, GROUPS * UNIT], U32, name="c_gate", align_bytes=64)
+            s_gate = work.tile([P, GROUPS * UNIT], U8, name="s_gate", align_bytes=64)
+            c_up = work.tile([P, GROUPS * UNIT], U32, name="c_up", align_bytes=64)
+            s_up = work.tile([P, GROUPS * UNIT], U8, name="s_up", align_bytes=64)
+            nc.vector.quantize_mx(
+                out=c_gate[:].bitcast(FP8X4), scales=s_gate[:], in_=dgate[i][:].rearrange("p g c -> p (g c)")
+            )
+            nc.vector.quantize_mx(
+                out=c_up[:].bitcast(FP8X4), scales=s_up[:], in_=dup[i][:].rearrange("p g c -> p (g c)")
+            )
+            codes[i] = ((c_up, s_up), (c_gate, s_gate))
+
+        banks = {}
+
+        def second_matmuls(i):
+            for k in range(2):
+                c, s = codes[i][k]
+                bank = out_pool.tile([P, D], F32, tag="out")
+                for g in range(GROUPS):
+                    nc.tensor.matmul_mx(
+                        out=bank[:],
+                        lhsT=c[:, UNIT * g : UNIT * (g + 1)].bitcast(FP8X4),
+                        lhsT_scale=s[:, UNIT * g : UNIT * (g + 1)],
+                        rhs=x_codes[:, g, :].bitcast(FP8X4),
+                        rhs_scale=x_scales[:, g, :],
+                        start=(g == 0),
+                        stop=(g == GROUPS - 1),
+                    )
+                banks[i, k] = bank
+
+        def store(i, k):
+            res = results.tile([P, D], F32, name=f"res{k}")
+            nc.scalar.activation(out=res[:], in_=banks[i, k][:], func=ACT.Copy, scale=factor[:, k : k + 1])
+            nc.sync.dma_start(out=(out_0, out_1)[k][UNIT * i : UNIT * (i + 1), :], in_=res[:])
+
+        sums = keep.tile([P, GROUPS], F32)
+        square_junk = keep.tile([P, PACK * D], BF16)
+        mean2 = keep.tile([P, 1], F32)
+        mag = keep.tile([P, 1], F32)
+        ema = keep.tile([P, 1], F32)
+        inv = keep.tile([P, 1], F32)
+        ratio = keep.tile([P, 1], F32)
+        factor = keep.tile([P, 2], F32)
+
+        def square_err(g):
+            nc.scalar.activation(
+                out=square_junk[:], in_=err_raw[g][:].rearrange("p t k -> p (t k)"), func=ACT.Square, accum_out=sums[:, g : g + 1]
+            )
+
+        def total_of_squares():
+            bank = out_pool.tile([P, D], F32, tag="out")
+            for g in range(GROUPS):
+                nc.tensor.matmul(bank[:, 0:1], ones[:], sums[:, g : g + 1], start=(g == 0), stop=(g == GROUPS - 1))
+            nc.vector.tensor_scalar(out=mean2[:], in0=bank[:, 0:1], scalar1=1.0 / (TOKENS * TOKENS), scalar2=None, op0=ALU.mult)
+            nc.gpsimd.tensor_tensor(out=mag[:], in0=mean2[:], in1=half[:], op=ALU.pow)
+
+        def surprise_factor():
+            nc.vector.tensor_scalar(out=ema[:], in0=mag[:], scalar1=0.05, scalar2=0.95, op0=ALU.mult, op1=ALU.add)
+            nc.vector.tensor_scalar(out=ema[:], in0=ema[:], scalar1=1e-8, scalar2=None, op0=ALU.max)
+            nc.vector.reciprocal(out=inv[:], in_=ema[:])
+            nc.vector.tensor_tensor(out=ratio[:], in0=mag[:], in1=inv[:], op=ALU.mult)
+            nc.vector.tensor_scalar(
+                out=factor[:, 0:1], in0=ratio[:], scalar1=3.0, scalar2=0.5 / TOKENS, op0=ALU.min, op1=ALU.mult
+            )
+            nc.vector.tensor_scalar(
+                out=factor[:, 1:2], in0=ratio[:], scalar1=3.0, scalar2=-0.5 / TOKENS, op0=ALU.min, op1=ALU.mult
+            )
+
+        gate_activations(0)
+        first_matmuls(0)
+        square_err(0)
+        square_err(1)
+        gate_activations(1)
+
+        for step in range(UNITS + 2):
+            if step >= 2:
+                second_matmuls(step - 2)
+            if step + 1 < UNITS:
+                first_matmuls(step + 1)
+            if step < UNITS:
+                psum_products(step)
+                up_product(step)
+            if step == 2:
+                surprise_factor()
+            if 1 <= step <= UNITS:
+                quantize(step - 1)
+            if step < UNITS:
+                gate_product(step)
+            if step == 1:
+                total_of_squares()
+            if step + 2 < UNITS:
+                gate_activations(step + 2)
+            if step >= 2:
+                store(step - 2, 0)
+                store(step - 2, 1)

@@ -133,12 +133,6 @@ def tile_continuummemorysystem_pa_w8_kernel(
             nc.vector.tensor_scalar(
                 out=x_wide[:, j, :], in0=x_raw[:, j, :].bitcast(FP8), scalar1=xs[:, j : j + 1], scalar2=None, op0=ALU.mult
             )
-        for g in range(GROUPS):
-            nc.vector.tensor_copy(
-                out=x_grouped[:, g].rearrange("p (c i) t -> p c t i", i=4),
-                in_=x_wide[:, PACK * g : PACK * (g + 1), :].rearrange("p t (c i) -> p c t i", i=4),
-            )
-
         err_grouped = [keep.tile([P, PACK, P, PACK], BF16, align_bytes=64, name=f"err_grouped{g}") for g in range(GROUPS)]
         err_codes = keep.tile([P, GROUPS, PACK * P], U32, align_bytes=64)
         err_scales = keep.tile([P, GROUPS, PACK * P], U8, align_bytes=64)
@@ -151,7 +145,7 @@ def tile_continuummemorysystem_pa_w8_kernel(
                     words = err_raw[g][:, 2 * pair + s, :].bitcast(F32)
                     for u in range(2):
                         nc.tensor.transpose(bank[:, s, u, :], words[:, u : D // 2 : 2], ident_f32[:])
-                nc.scalar.copy(
+                nc.vector.tensor_copy(
                     out=err_grouped[g][:, 2 * pair : 2 * pair + 2].rearrange("p s r e -> p s (r e)").bitcast(F32).rearrange(
                         "p s (r u) -> p s r u", u=2
                     ),
@@ -162,24 +156,34 @@ def tile_continuummemorysystem_pa_w8_kernel(
                 scales=err_scales[:, g, :],
                 in_=err_grouped[g][:].rearrange("p t r e -> p (t r e)"),
             )
+            nc.vector.tensor_copy(
+                out=x_grouped[:, g].rearrange("p (c i) t -> p c t i", i=4),
+                in_=x_wide[:, PACK * g : PACK * (g + 1), :].rearrange("p t (c i) -> p c t i", i=4),
+            )
+        for g in range(GROUPS):
             nc.vector.quantize_mx(
                 out=x_codes[:, g, :].bitcast(FP8X4),
                 scales=x_scales[:, g, :],
                 in_=x_grouped[:, g].rearrange("p n t -> p (n t)"),
             )
 
-        th, sl, dh, uu, p2, yy, dup, dgate, codes = {}, {}, {}, {}, {}, {}, {}, {}, {}
+        th, si, sl, dh, uu, p2, yy, dup, dgate, codes = {}, {}, {}, {}, {}, {}, {}, {}, {}, {}
 
         def column_block(tiles, i):
             c, off = locate(chunk_starts, CHUNKS, UNIT * i)
             return tiles[c][:, :, off : off + UNIT]
 
-        def gate_activations(i):
-            g_view = column_block(gate_tiles, i).rearrange("p (g t) n -> p g n t", t=PACK)
-            th[i] = acts.tile([P, GROUPS, UNIT, PACK], F32, name="th")
-            sl[i] = acts.tile([P, GROUPS, UNIT, PACK], F32, name="sl")
-            nc.scalar.activation(out=th[i][:], in_=g_view, func=ACT.Tanh, scale=0.5)
-            nc.scalar.activation(out=sl[i][:], in_=g_view, func=ACT.Silu, scale=-1.0)
+        def tanh_part(i):
+            th[i] = acts.tile([P, GROUPS * PACK, UNIT], F32, name="th")
+            nc.scalar.activation(out=th[i][:], in_=column_block(gate_tiles, i), func=ACT.Tanh, scale=0.5)
+
+        def silu_part(i):
+            si[i] = acts.tile([P, GROUPS * PACK, UNIT], F32, name="si")
+            nc.scalar.activation(out=si[i][:], in_=column_block(gate_tiles, i), func=ACT.Silu)
+
+        def mirrored_part(i):
+            sl[i] = acts.tile([P, GROUPS * PACK, UNIT], F32, name="sl")
+            nc.scalar.activation(out=sl[i][:], in_=column_block(gate_tiles, i), func=ACT.Silu, scale=-1.0)
 
         def first_matmuls(i):
             c, off = locate(w_starts, W_CHUNKS, UNIT * i)
@@ -196,6 +200,8 @@ def tile_continuummemorysystem_pa_w8_kernel(
                         stop=True,
                     )
                 dh[i, g] = bank
+
+        def up_to_psum(i):
             for g in range(GROUPS):
                 bank = u_pool.tile([P, PACK, UNIT], F32, tag="uu")
                 nc.tensor.matmul(
@@ -203,42 +209,39 @@ def tile_continuummemorysystem_pa_w8_kernel(
                 )
                 uu[i, g] = bank
 
-        def psum_products(i):
-            p2[i] = work.tile([P, GROUPS, UNIT * PACK], F32, name="p2")
-            yy[i] = work.tile([P, GROUPS, UNIT * PACK], F32, name="yy")
+        def slots(g):
+            return slice(PACK * g, PACK * (g + 1))
+
+        def d_h_products(i):
+            p2[i] = work.tile([P, GROUPS * PACK, UNIT], F32, name="p2")
+            dup[i] = work.tile([P, GROUPS, UNIT * PACK], BF16, name="dup", align_bytes=64)
             for g in range(GROUPS):
                 nc.vector.scalar_tensor_tensor(
-                    out=p2[i][:, g].rearrange("p (n t) -> p n t", t=PACK),
-                    in0=th[i][:, g],
-                    scalar=1.0,
-                    in1=dh[i, g][:].rearrange("p t n -> p n t"),
-                    op0=ALU.add,
-                    op1=ALU.mult,
+                    out=p2[i][:, slots(g), :], in0=th[i][:, slots(g), :], scalar=1.0, in1=dh[i, g][:], op0=ALU.add, op1=ALU.mult
                 )
-            for g in range(GROUPS):
-                nc.vector.scalar_tensor_tensor(
-                    out=yy[i][:, g].rearrange("p (n t) -> p n t", t=PACK),
-                    in0=sl[i][:, g],
-                    scalar=-1.0,
-                    in1=uu[i, g][:].rearrange("p t n -> p n t"),
-                    op0=ALU.add,
-                    op1=ALU.mult,
+                nc.vector.tensor_tensor(
+                    out=dup[i][:, g].rearrange("p (c i t) -> p c t i", i=4, t=PACK),
+                    in0=dh[i, g][:].rearrange("p t (c i) -> p c t i", i=4),
+                    in1=si[i][:, slots(g), :].rearrange("p t (c i) -> p c t i", i=4),
+                    op=ALU.mult,
                 )
 
-        def up_product(i):
-            dup[i] = work.tile([P, GROUPS, UNIT * PACK], BF16, name="dup", align_bytes=64)
-            g_view = column_block(gate_tiles, i).rearrange("p (g t) n -> p g n t", t=PACK)
+        def up_products(i):
+            yy[i] = work.tile([P, GROUPS * PACK, UNIT], F32, name="yy")
             for g in range(GROUPS):
-                nc.gpsimd.tensor_tensor(
-                    out=dup[i][:, g].rearrange("p (n t) -> p n t", t=PACK),
-                    in0=p2[i][:, g].rearrange("p (n t) -> p n t", t=PACK),
-                    in1=g_view[:, g],
-                    op=ALU.mult,
+                nc.vector.scalar_tensor_tensor(
+                    out=yy[i][:, slots(g), :], in0=sl[i][:, slots(g), :], scalar=-1.0, in1=uu[i, g][:], op0=ALU.add, op1=ALU.mult
                 )
 
         def gate_product(i):
             dgate[i] = work.tile([P, GROUPS, UNIT * PACK], BF16, name="dgate", align_bytes=64)
-            nc.vector.tensor_tensor(out=dgate[i][:], in0=p2[i][:], in1=yy[i][:], op=ALU.mult)
+            for g in range(GROUPS):
+                nc.gpsimd.tensor_tensor(
+                    out=dgate[i][:, g].rearrange("p (n t) -> p n t", t=PACK),
+                    in0=p2[i][:, slots(g), :].rearrange("p t n -> p n t"),
+                    in1=yy[i][:, slots(g), :].rearrange("p t n -> p n t"),
+                    op=ALU.mult,
+                )
 
         def quantize(i):
             c_gate = work.tile([P, GROUPS * UNIT], U32, name="c_gate", align_bytes=64)
@@ -246,10 +249,10 @@ def tile_continuummemorysystem_pa_w8_kernel(
             c_up = work.tile([P, GROUPS * UNIT], U32, name="c_up", align_bytes=64)
             s_up = work.tile([P, GROUPS * UNIT], U8, name="s_up", align_bytes=64)
             nc.vector.quantize_mx(
-                out=c_gate[:].bitcast(FP8X4), scales=s_gate[:], in_=dgate[i][:].rearrange("p g c -> p (g c)")
+                out=c_up[:].bitcast(FP8X4), scales=s_up[:], in_=dup[i][:].rearrange("p g c -> p (g c)")
             )
             nc.vector.quantize_mx(
-                out=c_up[:].bitcast(FP8X4), scales=s_up[:], in_=dup[i][:].rearrange("p g c -> p (g c)")
+                out=c_gate[:].bitcast(FP8X4), scales=s_gate[:], in_=dgate[i][:].rearrange("p g c -> p (g c)")
             )
             codes[i] = ((c_up, s_up), (c_gate, s_gate))
 
@@ -273,7 +276,10 @@ def tile_continuummemorysystem_pa_w8_kernel(
 
         def store(i, k):
             res = results.tile([P, D], F32, name=f"res{k}")
-            nc.scalar.activation(out=res[:], in_=banks[i, k][:], func=ACT.Copy, scale=factor[:, k : k + 1])
+            if k == 1 and i % 2 == 1:
+                nc.vector.tensor_scalar(out=res[:], in0=banks[i, k][:], scalar1=factor[:, k : k + 1], scalar2=None, op0=ALU.mult)
+            else:
+                nc.scalar.activation(out=res[:], in_=banks[i, k][:], func=ACT.Copy, scale=factor[:, k : k + 1])
             nc.sync.dma_start(out=(out_0, out_1)[k][UNIT * i : UNIT * (i + 1), :], in_=res[:])
 
         sums = keep.tile([P, GROUPS], F32)
@@ -303,36 +309,45 @@ def tile_continuummemorysystem_pa_w8_kernel(
             nc.vector.reciprocal(out=inv[:], in_=ema[:])
             nc.vector.tensor_tensor(out=ratio[:], in0=mag[:], in1=inv[:], op=ALU.mult)
             nc.vector.tensor_scalar(
-                out=factor[:, 0:1], in0=ratio[:], scalar1=3.0, scalar2=0.5 / TOKENS, op0=ALU.min, op1=ALU.mult
+                out=factor[:, 0:1], in0=ratio[:], scalar1=3.0, scalar2=1.0 / TOKENS, op0=ALU.min, op1=ALU.mult
             )
             nc.vector.tensor_scalar(
                 out=factor[:, 1:2], in0=ratio[:], scalar1=3.0, scalar2=-0.5 / TOKENS, op0=ALU.min, op1=ALU.mult
             )
 
-        gate_activations(0)
-        first_matmuls(0)
         square_err(0)
         square_err(1)
-        gate_activations(1)
+        tanh_part(0)
+        silu_part(0)
+        mirrored_part(0)
+        first_matmuls(0)
+        up_to_psum(0)
+        tanh_part(1)
+        silu_part(1)
+        mirrored_part(1)
 
         for step in range(UNITS + 2):
             if step >= 2:
-                second_matmuls(step - 2)
+                store(step - 2, 0)
+                store(step - 2, 1)
             if step + 1 < UNITS:
                 first_matmuls(step + 1)
             if step < UNITS:
-                psum_products(step)
-                up_product(step)
-            if step == 2:
+                d_h_products(step)
+            if step == 1:
                 surprise_factor()
             if 1 <= step <= UNITS:
                 quantize(step - 1)
+                second_matmuls(step - 1)
+            if step + 1 < UNITS:
+                up_to_psum(step + 1)
+            if step < UNITS:
+                up_products(step)
+            if step == 0:
+                total_of_squares()
             if step < UNITS:
                 gate_product(step)
-            if step == 1:
-                total_of_squares()
             if step + 2 < UNITS:
-                gate_activations(step + 2)
-            if step >= 2:
-                store(step - 2, 0)
-                store(step - 2, 1)
+                tanh_part(step + 2)
+                silu_part(step + 2)
+                mirrored_part(step + 2)

@@ -24,6 +24,7 @@ UNIT = 128
 UNITS = H // UNIT
 CHUNKS = (256, 256, 512, 512, 512)
 W_CHUNKS = (256, 768, 1024)
+GATE_IN_PSUM = tuple(i % 2 == 1 for i in range(UNITS))
 
 
 def starts_of(widths):
@@ -75,8 +76,10 @@ def tile_continuummemorysystem_pa_w8_kernel(
         x_raw = keep.tile([P, GROUPS * PACK, D], U8, align_bytes=64)
         xs = keep.tile([P, GROUPS * PACK], F32)
         x_view = x_bytes.rearrange("(g p t) n -> g p t n", p=P, t=PACK)
-        for g in range(GROUPS):
+        def load_x(g):
             nc.sync.dma_start(out=x_raw[:, PACK * g : PACK * (g + 1), :], in_=x_view[g])
+
+        load_x(0)
         nc.sync.dma_start(
             out=xs[:].rearrange("p (g t) -> p g t", t=PACK), in_=x_scale.rearrange("(g p t) o -> p g (t o)", p=P, t=PACK)
         )
@@ -87,12 +90,6 @@ def tile_continuummemorysystem_pa_w8_kernel(
             e = keep.tile([P, PACK, D], BF16, name=f"err_raw{g}")
             nc.sync.dma_start(out=e[:], in_=err_view[g])
             err_raw.append(e)
-
-        for q in range(4):
-            nc.sync.dma_start(
-                out=planes[32 * q : 32 * q + 4, :].bitcast(I32),
-                in_=w_scales[0, 4 * q : 4 * q + 4, :].bitcast(I32),
-            )
 
         w_flat = w_words[0].rearrange("p n t -> p (n t)")
         w_tiles = [keep.tile([P, w], U32, align_bytes=64, name=f"w{c}") for c, w in enumerate(W_CHUNKS)]
@@ -115,8 +112,14 @@ def tile_continuummemorysystem_pa_w8_kernel(
                     out=tiles[c][:, PACK * g : PACK * (g + 1), :], in_=view[g][:, :, a : a + w]
                 )
 
-        load_w(0)
+        load_x(1)
         load_h(gate_view, gate_tiles, 0)
+        load_w(0)
+        for q in range(4):
+            nc.sync.dma_start(
+                out=planes[32 * q : 32 * q + 4, :].bitcast(I32),
+                in_=w_scales[0, 4 * q : 4 * q + 4, :].bitcast(I32),
+            )
         load_h(up_view, up_tiles, 0)
         load_h(gate_view, gate_tiles, 1)
         load_h(up_view, up_tiles, 1)
@@ -129,15 +132,36 @@ def tile_continuummemorysystem_pa_w8_kernel(
 
         x_wide = keep.tile([P, GROUPS * PACK, D], BF16)
         x_grouped = keep.tile([P, GROUPS, D, PACK], BF16, align_bytes=64)
-        for j in range(GROUPS * PACK):
-            nc.vector.tensor_scalar(
-                out=x_wide[:, j, :], in0=x_raw[:, j, :].bitcast(FP8), scalar1=xs[:, j : j + 1], scalar2=None, op0=ALU.mult
+        x_codes = keep.tile([P, GROUPS, D], U32, align_bytes=64)
+        x_scales = keep.tile([P, GROUPS, D], U8, align_bytes=64)
+
+        def widen_x(g):
+            for j in range(PACK * g, PACK * (g + 1)):
+                nc.vector.tensor_scalar(
+                    out=x_wide[:, j, :], in0=x_raw[:, j, :].bitcast(FP8), scalar1=xs[:, j : j + 1], scalar2=None, op0=ALU.mult
+                )
+            for n in range(0, D, P):
+                nc.gpsimd.tensor_scalar(
+                    out=x_grouped[:, g, n : n + P, :],
+                    in0=x_wide[:, PACK * g : PACK * (g + 1), n : n + P].rearrange("p t n -> p n t"),
+                    scalar1=1.0,
+                    scalar2=0.0,
+                    op0=ALU.mult,
+                    op1=ALU.add,
+                )
+
+        def quantize_x(g):
+            nc.vector.quantize_mx(
+                out=x_codes[:, g, :].bitcast(FP8X4),
+                scales=x_scales[:, g, :],
+                in_=x_grouped[:, g].rearrange("p n t -> p (n t)"),
             )
+
+        widen_x(0)
+
         err_grouped = [keep.tile([P, PACK, P, PACK], BF16, align_bytes=64, name=f"err_grouped{g}") for g in range(GROUPS)]
         err_codes = keep.tile([P, GROUPS, PACK * P], U32, align_bytes=64)
         err_scales = keep.tile([P, GROUPS, PACK * P], U8, align_bytes=64)
-        x_codes = keep.tile([P, GROUPS, D], U32, align_bytes=64)
-        x_scales = keep.tile([P, GROUPS, D], U8, align_bytes=64)
         for g in range(GROUPS):
             for pair in range(2):
                 bank = out_pool.tile([P, 2, 2, P], F32, tag="out")
@@ -156,16 +180,8 @@ def tile_continuummemorysystem_pa_w8_kernel(
                 scales=err_scales[:, g, :],
                 in_=err_grouped[g][:].rearrange("p t r e -> p (t r e)"),
             )
-            nc.vector.tensor_copy(
-                out=x_grouped[:, g].rearrange("p (c i) t -> p c t i", i=4),
-                in_=x_wide[:, PACK * g : PACK * (g + 1), :].rearrange("p t (c i) -> p c t i", i=4),
-            )
-        for g in range(GROUPS):
-            nc.vector.quantize_mx(
-                out=x_codes[:, g, :].bitcast(FP8X4),
-                scales=x_scales[:, g, :],
-                in_=x_grouped[:, g].rearrange("p n t -> p (n t)"),
-            )
+
+        widen_x(1)
 
         th, si, sl, dh, uu, p2, yy, dup, dgate, codes = {}, {}, {}, {}, {}, {}, {}, {}, {}, {}
 
@@ -173,17 +189,21 @@ def tile_continuummemorysystem_pa_w8_kernel(
             c, off = locate(chunk_starts, CHUNKS, UNIT * i)
             return tiles[c][:, :, off : off + UNIT]
 
+        def interleaved(block):
+            return block.rearrange("p (g t) n -> p g n t", t=PACK)
+
         def tanh_part(i):
-            th[i] = acts.tile([P, GROUPS * PACK, UNIT], F32, name="th")
-            nc.scalar.activation(out=th[i][:], in_=column_block(gate_tiles, i), func=ACT.Tanh, scale=0.5)
+            th[i] = acts.tile([P, GROUPS, UNIT, PACK], F32, name="th")
+            nc.scalar.activation(out=th[i][:], in_=interleaved(column_block(gate_tiles, i)), func=ACT.Tanh, scale=0.5)
 
         def silu_part(i):
-            si[i] = acts.tile([P, GROUPS * PACK, UNIT], F32, name="si")
-            nc.scalar.activation(out=si[i][:], in_=column_block(gate_tiles, i), func=ACT.Silu)
+            if not GATE_IN_PSUM[i]:
+                si[i] = acts.tile([P, GROUPS, UNIT, PACK], F32, name="si")
+                nc.scalar.activation(out=si[i][:], in_=interleaved(column_block(gate_tiles, i)), func=ACT.Silu)
 
         def mirrored_part(i):
-            sl[i] = acts.tile([P, GROUPS * PACK, UNIT], F32, name="sl")
-            nc.scalar.activation(out=sl[i][:], in_=column_block(gate_tiles, i), func=ACT.Silu, scale=-1.0)
+            sl[i] = acts.tile([P, GROUPS, UNIT, PACK], F32, name="sl")
+            nc.scalar.activation(out=sl[i][:], in_=interleaved(column_block(gate_tiles, i)), func=ACT.Silu, scale=-1.0)
 
         def first_matmuls(i):
             c, off = locate(w_starts, W_CHUNKS, UNIT * i)
@@ -201,47 +221,47 @@ def tile_continuummemorysystem_pa_w8_kernel(
                     )
                 dh[i, g] = bank
 
-        def up_to_psum(i):
+        def copy_to_psum(i):
+            source = column_block(gate_tiles if GATE_IN_PSUM[i] else up_tiles, i)
             for g in range(GROUPS):
                 bank = u_pool.tile([P, PACK, UNIT], F32, tag="uu")
-                nc.tensor.matmul(
-                    bank[:], ident_bf[:], column_block(up_tiles, i)[:, PACK * g : PACK * (g + 1), :], start=True, stop=True
-                )
+                nc.tensor.matmul(bank[:], ident_bf[:], source[:, PACK * g : PACK * (g + 1), :], start=True, stop=True)
                 uu[i, g] = bank
 
-        def slots(g):
-            return slice(PACK * g, PACK * (g + 1))
+        def in_order(bank):
+            return bank[:].rearrange("p t n -> p n t")
+
+        def half_sigmoid_product(i, g):
+            nc.vector.scalar_tensor_tensor(
+                out=p2[i][:, g], in0=th[i][:, g], scalar=1.0, in1=in_order(dh[i, g]), op0=ALU.add, op1=ALU.mult
+            )
 
         def d_h_products(i):
-            p2[i] = work.tile([P, GROUPS * PACK, UNIT], F32, name="p2")
-            dup[i] = work.tile([P, GROUPS, UNIT * PACK], BF16, name="dup", align_bytes=64)
-            for g in range(GROUPS):
-                nc.vector.scalar_tensor_tensor(
-                    out=p2[i][:, slots(g), :], in0=th[i][:, slots(g), :], scalar=1.0, in1=dh[i, g][:], op0=ALU.add, op1=ALU.mult
-                )
-                nc.vector.tensor_tensor(
-                    out=dup[i][:, g].rearrange("p (c i t) -> p c t i", i=4, t=PACK),
-                    in0=dh[i, g][:].rearrange("p t (c i) -> p c t i", i=4),
-                    in1=si[i][:, slots(g), :].rearrange("p t (c i) -> p c t i", i=4),
-                    op=ALU.mult,
-                )
+            p2[i] = work.tile([P, GROUPS, UNIT, PACK], F32, name="p2")
+            dup[i] = work.tile([P, GROUPS, UNIT, PACK], BF16, name="dup", align_bytes=64)
+            if GATE_IN_PSUM[i]:
+                for g in range(GROUPS):
+                    half_sigmoid_product(i, g)
+                for g in range(GROUPS):
+                    nc.vector.tensor_tensor(out=dup[i][:, g], in0=p2[i][:, g], in1=in_order(uu[i, g]), op=ALU.mult)
+            else:
+                for g in range(GROUPS):
+                    half_sigmoid_product(i, g)
+                    nc.vector.tensor_tensor(out=dup[i][:, g], in0=in_order(dh[i, g]), in1=si[i][:, g], op=ALU.mult)
 
         def up_products(i):
-            yy[i] = work.tile([P, GROUPS * PACK, UNIT], F32, name="yy")
+            yy[i] = work.tile([P, GROUPS, UNIT, PACK], F32, name="yy")
             for g in range(GROUPS):
+                up = column_block(up_tiles, i)[:, PACK * g : PACK * (g + 1), :].rearrange("p t n -> p n t") if GATE_IN_PSUM[i] else in_order(uu[i, g])
                 nc.vector.scalar_tensor_tensor(
-                    out=yy[i][:, slots(g), :], in0=sl[i][:, slots(g), :], scalar=-1.0, in1=uu[i, g][:], op0=ALU.add, op1=ALU.mult
+                    out=yy[i][:, g], in0=sl[i][:, g], scalar=-1.0, in1=up, op0=ALU.add, op1=ALU.mult
                 )
 
         def gate_product(i):
-            dgate[i] = work.tile([P, GROUPS, UNIT * PACK], BF16, name="dgate", align_bytes=64)
+            dgate[i] = work.tile([P, GROUPS, UNIT, PACK], BF16, name="dgate", align_bytes=64)
+            engine = nc.vector if i == UNITS - 1 else nc.gpsimd
             for g in range(GROUPS):
-                nc.gpsimd.tensor_tensor(
-                    out=dgate[i][:, g].rearrange("p (n t) -> p n t", t=PACK),
-                    in0=p2[i][:, slots(g), :].rearrange("p t n -> p n t"),
-                    in1=yy[i][:, slots(g), :].rearrange("p t n -> p n t"),
-                    op=ALU.mult,
-                )
+                engine.tensor_tensor(out=dgate[i][:, g], in0=p2[i][:, g], in1=yy[i][:, g], op=ALU.mult)
 
         def quantize(i):
             c_gate = work.tile([P, GROUPS * UNIT], U32, name="c_gate", align_bytes=64)
@@ -249,10 +269,10 @@ def tile_continuummemorysystem_pa_w8_kernel(
             c_up = work.tile([P, GROUPS * UNIT], U32, name="c_up", align_bytes=64)
             s_up = work.tile([P, GROUPS * UNIT], U8, name="s_up", align_bytes=64)
             nc.vector.quantize_mx(
-                out=c_up[:].bitcast(FP8X4), scales=s_up[:], in_=dup[i][:].rearrange("p g c -> p (g c)")
+                out=c_up[:].bitcast(FP8X4), scales=s_up[:], in_=dup[i][:].rearrange("p g n t -> p (g n t)")
             )
             nc.vector.quantize_mx(
-                out=c_gate[:].bitcast(FP8X4), scales=s_gate[:], in_=dgate[i][:].rearrange("p g c -> p (g c)")
+                out=c_gate[:].bitcast(FP8X4), scales=s_gate[:], in_=dgate[i][:].rearrange("p g n t -> p (g n t)")
             )
             codes[i] = ((c_up, s_up), (c_gate, s_gate))
 
@@ -276,10 +296,8 @@ def tile_continuummemorysystem_pa_w8_kernel(
 
         def store(i, k):
             res = results.tile([P, D], F32, name=f"res{k}")
-            if k == 1 and i % 2 == 1:
-                nc.vector.tensor_scalar(out=res[:], in0=banks[i, k][:], scalar1=factor[:, k : k + 1], scalar2=None, op0=ALU.mult)
-            else:
-                nc.scalar.activation(out=res[:], in_=banks[i, k][:], func=ACT.Copy, scale=factor[:, k : k + 1])
+            c = 2 if k == 0 and GATE_IN_PSUM[i] else k
+            nc.scalar.activation(out=res[:], in_=banks[i, k][:], func=ACT.Copy, scale=factor[:, c : c + 1])
             nc.sync.dma_start(out=(out_0, out_1)[k][UNIT * i : UNIT * (i + 1), :], in_=res[:])
 
         sums = keep.tile([P, GROUPS], F32)
@@ -289,7 +307,7 @@ def tile_continuummemorysystem_pa_w8_kernel(
         ema = keep.tile([P, 1], F32)
         inv = keep.tile([P, 1], F32)
         ratio = keep.tile([P, 1], F32)
-        factor = keep.tile([P, 2], F32)
+        factor = keep.tile([P, 3], F32)
 
         def square_err(g):
             nc.scalar.activation(
@@ -314,39 +332,45 @@ def tile_continuummemorysystem_pa_w8_kernel(
             nc.vector.tensor_scalar(
                 out=factor[:, 1:2], in0=ratio[:], scalar1=3.0, scalar2=-0.5 / TOKENS, op0=ALU.min, op1=ALU.mult
             )
+            nc.vector.tensor_scalar(
+                out=factor[:, 2:3], in0=ratio[:], scalar1=3.0, scalar2=0.5 / TOKENS, op0=ALU.min, op1=ALU.mult
+            )
 
         square_err(0)
-        square_err(1)
         tanh_part(0)
         silu_part(0)
         mirrored_part(0)
         first_matmuls(0)
-        up_to_psum(0)
+        copy_to_psum(0)
+        square_err(1)
         tanh_part(1)
         silu_part(1)
         mirrored_part(1)
 
         for step in range(UNITS + 2):
-            if step >= 2:
-                store(step - 2, 0)
-                store(step - 2, 1)
             if step + 1 < UNITS:
                 first_matmuls(step + 1)
             if step < UNITS:
                 d_h_products(step)
             if step == 1:
+                quantize_x(0)
+                quantize_x(1)
+            if step == 2:
                 surprise_factor()
             if 1 <= step <= UNITS:
                 quantize(step - 1)
                 second_matmuls(step - 1)
-            if step + 1 < UNITS:
-                up_to_psum(step + 1)
             if step < UNITS:
                 up_products(step)
-            if step == 0:
+            if step + 1 < UNITS:
+                copy_to_psum(step + 1)
+            if step == 1:
                 total_of_squares()
             if step < UNITS:
                 gate_product(step)
+            if step >= 2:
+                store(step - 2, 0)
+                store(step - 2, 1)
             if step + 2 < UNITS:
                 tanh_part(step + 2)
                 silu_part(step + 2)

@@ -24,7 +24,8 @@ UNIT = 128
 UNITS = H // UNIT
 CHUNKS = (256, 256, 512, 512, 512)
 W_CHUNKS = (256, 768, 1024)
-GATE_IN_PSUM = tuple(i % 2 == 1 for i in range(UNITS))
+PAIRS = UNITS // 2
+BOTH_IN_PSUM = (0, 1, 2)
 
 
 def starts_of(widths):
@@ -50,12 +51,12 @@ def tile_continuummemorysystem_pa_w8_kernel(
 
     with ExitStack() as ctx:
         keep = ctx.enter_context(tc.tile_pool(name="keep", bufs=1))
-        acts = ctx.enter_context(tc.tile_pool(name="acts", bufs=3))
-        work = ctx.enter_context(tc.tile_pool(name="work", bufs=2))
-        results = ctx.enter_context(tc.tile_pool(name="results", bufs=5))
-        dh_pool = ctx.enter_context(tc.psum_pool(name="dh_pool", bufs=3))
-        u_pool = ctx.enter_context(tc.psum_pool(name="u_pool", bufs=2))
-        out_pool = ctx.enter_context(tc.psum_pool(name="out_pool", bufs=3))
+        acts = ctx.enter_context(tc.tile_pool(name="acts", bufs=4))
+        work = ctx.enter_context(tc.tile_pool(name="work", bufs=3))
+        results = ctx.enter_context(tc.tile_pool(name="results", bufs=4))
+        dh_pool = ctx.enter_context(tc.psum_pool(name="dh_pool", bufs=4))
+        copy_pool = ctx.enter_context(tc.psum_pool(name="copy_pool", bufs=2))
+        out_pool = ctx.enter_context(tc.psum_pool(name="out_pool", bufs=2))
         ctx.enter_context(tc.manual_schedule())
 
         one_col = keep.tile([P, 1], F32)
@@ -140,7 +141,12 @@ def tile_continuummemorysystem_pa_w8_kernel(
                 nc.vector.tensor_scalar(
                     out=x_wide[:, j, :], in0=x_raw[:, j, :].bitcast(FP8), scalar1=xs[:, j : j + 1], scalar2=None, op0=ALU.mult
                 )
-            for n in range(0, D, P):
+            if g == 0:
+                nc.vector.tensor_copy(
+                    out=x_grouped[:, g].rearrange("p (c i) t -> p c t i", i=4),
+                    in_=x_wide[:, PACK * g : PACK * (g + 1), :].rearrange("p t (c i) -> p c t i", i=4),
+                )
+            for n in range(0, D if g == 1 else 0, P):
                 nc.gpsimd.tensor_scalar(
                     out=x_grouped[:, g, n : n + P, :],
                     in0=x_wide[:, PACK * g : PACK * (g + 1), n : n + P].rearrange("p t n -> p n t"),
@@ -160,6 +166,18 @@ def tile_continuummemorysystem_pa_w8_kernel(
         widen_x(0)
 
         err_grouped = [keep.tile([P, PACK, P, PACK], BF16, align_bytes=64, name=f"err_grouped{g}") for g in range(GROUPS)]
+        sums = keep.tile([P, 3], F32)
+        square_junk = keep.tile([P, PACK * D], BF16)
+
+        def square_err(part, g, first, last):
+            nc.scalar.activation(
+                out=square_junk[:, : D * (last - first)],
+                in_=err_raw[g][:, first:last, :].rearrange("p t k -> p (t k)"),
+                func=ACT.Square,
+                accum_out=sums[:, part : part + 1],
+            )
+
+        square_err(0, 0, 0, 2)
         err_codes = keep.tile([P, GROUPS, PACK * P], U32, align_bytes=64)
         err_scales = keep.tile([P, GROUPS, PACK * P], U8, align_bytes=64)
         for g in range(GROUPS):
@@ -169,7 +187,7 @@ def tile_continuummemorysystem_pa_w8_kernel(
                     words = err_raw[g][:, 2 * pair + s, :].bitcast(F32)
                     for u in range(2):
                         nc.tensor.transpose(bank[:, s, u, :], words[:, u : D // 2 : 2], ident_f32[:])
-                nc.vector.tensor_copy(
+                nc.scalar.copy(
                     out=err_grouped[g][:, 2 * pair : 2 * pair + 2].rearrange("p s r e -> p s (r e)").bitcast(F32).rearrange(
                         "p s (r u) -> p s r u", u=2
                     ),
@@ -180,30 +198,32 @@ def tile_continuummemorysystem_pa_w8_kernel(
                 scales=err_scales[:, g, :],
                 in_=err_grouped[g][:].rearrange("p t r e -> p (t r e)"),
             )
+            if g == 0:
+                widen_x(1)
 
-        widen_x(1)
-
-        th, si, sl, dh, uu, p2, yy, dup, dgate, codes = {}, {}, {}, {}, {}, {}, {}, {}, {}, {}
+        th, si, sl, dh, copied, p2, yy, dup, dgate, codes, banks = {}, {}, {}, {}, {}, {}, {}, {}, {}, {}, {}
 
         def column_block(tiles, i):
             c, off = locate(chunk_starts, CHUNKS, UNIT * i)
             return tiles[c][:, :, off : off + UNIT]
 
-        def interleaved(block):
-            return block.rearrange("p (g t) n -> p g n t", t=PACK)
+        def slots(g):
+            return slice(PACK * g, PACK * (g + 1))
+
+        def activation_of_gate(i, name, func, scale):
+            t = acts.tile([P, GROUPS, UNIT, PACK], F32, tag=name, name=name, bufs=2 if name == "si" else 4)
+            view = column_block(gate_tiles, i).rearrange("p (g t) n -> p g n t", t=PACK)
+            nc.scalar.activation(out=t[:], in_=view, func=func, scale=scale)
+            return t
 
         def tanh_part(i):
-            th[i] = acts.tile([P, GROUPS, UNIT, PACK], F32, name="th")
-            nc.scalar.activation(out=th[i][:], in_=interleaved(column_block(gate_tiles, i)), func=ACT.Tanh, scale=0.5)
-
-        def silu_part(i):
-            if not GATE_IN_PSUM[i]:
-                si[i] = acts.tile([P, GROUPS, UNIT, PACK], F32, name="si")
-                nc.scalar.activation(out=si[i][:], in_=interleaved(column_block(gate_tiles, i)), func=ACT.Silu)
+            th[i] = activation_of_gate(i, "th", ACT.Tanh, 0.5)
 
         def mirrored_part(i):
-            sl[i] = acts.tile([P, GROUPS, UNIT, PACK], F32, name="sl")
-            nc.scalar.activation(out=sl[i][:], in_=interleaved(column_block(gate_tiles, i)), func=ACT.Silu, scale=-1.0)
+            sl[i] = activation_of_gate(i, "sl", ACT.Silu, -1.0)
+
+        def silu_part(i):
+            si[i] = activation_of_gate(i, "si", ACT.Silu, 1.0)
 
         def first_matmuls(i):
             c, off = locate(w_starts, W_CHUNKS, UNIT * i)
@@ -221,87 +241,102 @@ def tile_continuummemorysystem_pa_w8_kernel(
                     )
                 dh[i, g] = bank
 
-        def copy_to_psum(i):
-            source = column_block(gate_tiles if GATE_IN_PSUM[i] else up_tiles, i)
+        def copy_to_psum(i, tiles):
+            bank = copy_pool.tile([P, GROUPS * PACK, UNIT], BF16, tag="copied")
+            source = column_block(tiles, i)
             for g in range(GROUPS):
-                bank = u_pool.tile([P, PACK, UNIT], F32, tag="uu")
-                nc.tensor.matmul(bank[:], ident_bf[:], source[:, PACK * g : PACK * (g + 1), :], start=True, stop=True)
-                uu[i, g] = bank
+                nc.tensor.matmul(bank[:, slots(g), :], ident_bf[:], source[:, slots(g), :], start=True, stop=True)
+            return bank
 
-        def in_order(bank):
-            return bank[:].rearrange("p t n -> p n t")
-
-        def half_sigmoid_product(i, g):
-            nc.vector.scalar_tensor_tensor(
-                out=p2[i][:, g], in0=th[i][:, g], scalar=1.0, in1=in_order(dh[i, g]), op0=ALU.add, op1=ALU.mult
-            )
-
-        def d_h_products(i):
+        def half_sigmoid_products(i):
             p2[i] = work.tile([P, GROUPS, UNIT, PACK], F32, name="p2")
-            dup[i] = work.tile([P, GROUPS, UNIT, PACK], BF16, name="dup", align_bytes=64)
-            if GATE_IN_PSUM[i]:
-                for g in range(GROUPS):
-                    half_sigmoid_product(i, g)
-                for g in range(GROUPS):
-                    nc.vector.tensor_tensor(out=dup[i][:, g], in0=p2[i][:, g], in1=in_order(uu[i, g]), op=ALU.mult)
-            else:
-                for g in range(GROUPS):
-                    half_sigmoid_product(i, g)
-                    nc.vector.tensor_tensor(out=dup[i][:, g], in0=in_order(dh[i, g]), in1=si[i][:, g], op=ALU.mult)
-
-        def up_products(i):
-            yy[i] = work.tile([P, GROUPS, UNIT, PACK], F32, name="yy")
             for g in range(GROUPS):
-                up = column_block(up_tiles, i)[:, PACK * g : PACK * (g + 1), :].rearrange("p t n -> p n t") if GATE_IN_PSUM[i] else in_order(uu[i, g])
                 nc.vector.scalar_tensor_tensor(
-                    out=yy[i][:, g], in0=sl[i][:, g], scalar=-1.0, in1=up, op0=ALU.add, op1=ALU.mult
+                    out=p2[i][:, g],
+                    in0=th[i][:, g],
+                    scalar=1.0,
+                    in1=dh[i, g][:].rearrange("p t n -> p n t"),
+                    op0=ALU.add,
+                    op1=ALU.mult,
                 )
 
-        def gate_product(i):
-            dgate[i] = work.tile([P, GROUPS, UNIT, PACK], BF16, name="dgate", align_bytes=64)
-            engine = nc.vector if i == UNITS - 1 else nc.gpsimd
+        def up_products(i, up, groups):
+            if 0 in groups:
+                yy[i] = work.tile([P, GROUPS, UNIT, PACK], F32, name="yy")
+            for g in groups:
+                nc.vector.scalar_tensor_tensor(
+                    out=yy[i][:, g],
+                    in0=sl[i][:, g],
+                    scalar=-1.0,
+                    in1=up[:, slots(g), :].rearrange("p t n -> p n t"),
+                    op0=ALU.add,
+                    op1=ALU.mult,
+                )
+
+        def d_up_from_d_h(i, out):
             for g in range(GROUPS):
-                engine.tensor_tensor(out=dgate[i][:, g], in0=p2[i][:, g], in1=yy[i][:, g], op=ALU.mult)
+                nc.vector.tensor_tensor(
+                    out=out[:, g], in0=dh[i, g][:].rearrange("p t n -> p n t"), in1=si[i][:, g], op=ALU.mult
+                )
 
-        def quantize(i):
-            c_gate = work.tile([P, GROUPS * UNIT], U32, name="c_gate", align_bytes=64)
-            s_gate = work.tile([P, GROUPS * UNIT], U8, name="s_gate", align_bytes=64)
-            c_up = work.tile([P, GROUPS * UNIT], U32, name="c_up", align_bytes=64)
-            s_up = work.tile([P, GROUPS * UNIT], U8, name="s_up", align_bytes=64)
-            nc.vector.quantize_mx(
-                out=c_up[:].bitcast(FP8X4), scales=s_up[:], in_=dup[i][:].rearrange("p g n t -> p (g n t)")
+        def d_up_from_gate(i, gate, out):
+            nc.vector.tensor_tensor(
+                out=out, in0=p2[i][:], in1=gate[:].rearrange("p (g t) n -> p g n t", t=PACK), op=ALU.mult
             )
-            nc.vector.quantize_mx(
-                out=c_gate[:].bitcast(FP8X4), scales=s_gate[:], in_=dgate[i][:].rearrange("p g n t -> p (g n t)")
+
+        def gate_product(engine, i, out):
+            engine.tensor_tensor(
+                out=out.rearrange("p g n t -> p (g n t)"),
+                in0=p2[i][:].rearrange("p g n t -> p (g n t)"),
+                in1=yy[i][:].rearrange("p g n t -> p (g n t)"),
+                op=ALU.mult,
             )
-            codes[i] = ((c_up, s_up), (c_gate, s_gate))
 
-        banks = {}
+        def pair_tile(name):
+            return work.tile([P, 2, GROUPS, UNIT, PACK], BF16, tag=name, name=name, align_bytes=64, bufs=2)
 
-        def second_matmuls(i):
-            for k in range(2):
-                c, s = codes[i][k]
+        def quantize(keys, values, name):
+            n = len(keys) * GROUPS * UNIT
+            c = work.tile([P, 2 * GROUPS * UNIT], U32, tag=name + "_codes", name="codes_tile", align_bytes=64, bufs=3)
+            s = work.tile([P, 2 * GROUPS * UNIT], U8, tag=name + "_scales", name="scales_tile", align_bytes=64, bufs=3)
+            nc.vector.quantize_mx(
+                out=c[:, :n].bitcast(FP8X4), scales=s[:, :n], in_=values.rearrange("p k g n t -> p (k g n t)")
+            )
+            for slot, key in enumerate(keys):
+                codes[key] = (c, s, slot * GROUPS * UNIT)
+
+        def second_matmuls(key, spare_bank):
+            c, s, base = codes[key]
+            if spare_bank:
+                bank = dh_pool.tile([P, D], F32, tag="dh")
+            else:
                 bank = out_pool.tile([P, D], F32, tag="out")
-                for g in range(GROUPS):
-                    nc.tensor.matmul_mx(
-                        out=bank[:],
-                        lhsT=c[:, UNIT * g : UNIT * (g + 1)].bitcast(FP8X4),
-                        lhsT_scale=s[:, UNIT * g : UNIT * (g + 1)],
-                        rhs=x_codes[:, g, :].bitcast(FP8X4),
-                        rhs_scale=x_scales[:, g, :],
-                        start=(g == 0),
-                        stop=(g == GROUPS - 1),
-                    )
-                banks[i, k] = bank
+            for g in range(GROUPS):
+                a = base + UNIT * g
+                nc.tensor.matmul_mx(
+                    out=bank[:],
+                    lhsT=c[:, a : a + UNIT].bitcast(FP8X4),
+                    lhsT_scale=s[:, a : a + UNIT],
+                    rhs=x_codes[:, g, :].bitcast(FP8X4),
+                    rhs_scale=x_scales[:, g, :],
+                    start=(g == 0),
+                    stop=(g == GROUPS - 1),
+                )
+            banks[key] = bank
 
-        def store(i, k):
-            res = results.tile([P, D], F32, name=f"res{k}")
-            c = 2 if k == 0 and GATE_IN_PSUM[i] else k
-            nc.scalar.activation(out=res[:], in_=banks[i, k][:], func=ACT.Copy, scale=factor[:, c : c + 1])
-            nc.sync.dma_start(out=(out_0, out_1)[k][UNIT * i : UNIT * (i + 1), :], in_=res[:])
+        def store(key, on_vector=False):
+            kind, i = key
+            res = results.tile([P, D], F32, tag="res", name="res", bufs=8)
+            column = 2 if kind == "gate" else 1 if i % 2 == 1 or i // 2 in BOTH_IN_PSUM else 0
+            if on_vector:
+                nc.vector.tensor_scalar(
+                    out=res[:], in0=banks[key][:], scalar1=factor[:, column : column + 1], scalar2=None, op0=ALU.mult
+                )
+            else:
+                nc.scalar.activation(out=res[:], in_=banks[key][:], func=ACT.Copy, scale=factor[:, column : column + 1])
+            out = out_1 if kind == "gate" else out_0
+            nc.sync.dma_start(out=out[UNIT * i : UNIT * (i + 1), :], in_=res[:])
 
-        sums = keep.tile([P, GROUPS], F32)
-        square_junk = keep.tile([P, PACK * D], BF16)
         mean2 = keep.tile([P, 1], F32)
         mag = keep.tile([P, 1], F32)
         ema = keep.tile([P, 1], F32)
@@ -309,15 +344,10 @@ def tile_continuummemorysystem_pa_w8_kernel(
         ratio = keep.tile([P, 1], F32)
         factor = keep.tile([P, 3], F32)
 
-        def square_err(g):
-            nc.scalar.activation(
-                out=square_junk[:], in_=err_raw[g][:].rearrange("p t k -> p (t k)"), func=ACT.Square, accum_out=sums[:, g : g + 1]
-            )
-
         def total_of_squares():
             bank = out_pool.tile([P, D], F32, tag="out")
-            for g in range(GROUPS):
-                nc.tensor.matmul(bank[:, 0:1], ones[:], sums[:, g : g + 1], start=(g == 0), stop=(g == GROUPS - 1))
+            for part in range(3):
+                nc.tensor.matmul(bank[:, 0:1], ones[:], sums[:, part : part + 1], start=(part == 0), stop=(part == 2))
             nc.vector.tensor_scalar(out=mean2[:], in0=bank[:, 0:1], scalar1=1.0 / (TOKENS * TOKENS), scalar2=None, op0=ALU.mult)
             nc.gpsimd.tensor_tensor(out=mag[:], in0=mean2[:], in1=half[:], op=ALU.pow)
 
@@ -326,52 +356,94 @@ def tile_continuummemorysystem_pa_w8_kernel(
             nc.vector.tensor_scalar(out=ema[:], in0=ema[:], scalar1=1e-8, scalar2=None, op0=ALU.max)
             nc.vector.reciprocal(out=inv[:], in_=ema[:])
             nc.vector.tensor_tensor(out=ratio[:], in0=mag[:], in1=inv[:], op=ALU.mult)
-            nc.vector.tensor_scalar(
-                out=factor[:, 0:1], in0=ratio[:], scalar1=3.0, scalar2=1.0 / TOKENS, op0=ALU.min, op1=ALU.mult
-            )
-            nc.vector.tensor_scalar(
-                out=factor[:, 1:2], in0=ratio[:], scalar1=3.0, scalar2=-0.5 / TOKENS, op0=ALU.min, op1=ALU.mult
-            )
-            nc.vector.tensor_scalar(
-                out=factor[:, 2:3], in0=ratio[:], scalar1=3.0, scalar2=0.5 / TOKENS, op0=ALU.min, op1=ALU.mult
-            )
+            for column, multiple in enumerate((1.0, 0.5, -0.5)):
+                nc.vector.tensor_scalar(
+                    out=factor[:, column : column + 1],
+                    in0=ratio[:],
+                    scalar1=3.0,
+                    scalar2=multiple / TOKENS,
+                    op0=ALU.min,
+                    op1=ALU.mult,
+                )
 
-        square_err(0)
-        tanh_part(0)
-        silu_part(0)
-        mirrored_part(0)
+        def even_copies(j):
+            up_copy[j] = copy_to_psum(2 * j, up_tiles)
+            if j in BOTH_IN_PSUM:
+                gate_copy[2 * j] = copy_to_psum(2 * j, gate_tiles)
+            else:
+                gate_copy[2 * j + 1] = copy_to_psum(2 * j + 1, gate_tiles)
+
+        def activations(j):
+            u, v = 2 * j, 2 * j + 1
+            parts = [(tanh_part, u), (mirrored_part, u), (tanh_part, v), (mirrored_part, v)]
+            if j not in BOTH_IN_PSUM:
+                parts = parts[:2] + [(silu_part, u)] + parts[2:]
+            return parts
+
+        up_copy, gate_copy = {}, {}
+        for part, i in activations(0):
+            part(i)
+        square_err(1, 0, 2, 4)
+        square_err(2, 1, 0, 4)
         first_matmuls(0)
-        copy_to_psum(0)
-        square_err(1)
-        tanh_part(1)
-        silu_part(1)
-        mirrored_part(1)
+        even_copies(0)
+        first_matmuls(1)
 
-        for step in range(UNITS + 2):
-            if step + 1 < UNITS:
-                first_matmuls(step + 1)
-            if step < UNITS:
-                d_h_products(step)
-            if step == 1:
+        pending = []
+        dgate[0] = pair_tile("dgate")
+        for j in range(PAIRS):
+            u, v = 2 * j, 2 * j + 1
+            more = j + 1 < PAIRS
+            dgate[j + 1] = pair_tile("dgate")
+            dup[j] = pair_tile("dup")
+
+            half_sigmoid_products(u)
+            if j == 1:
+                surprise_factor()
+            up_products(u, up_copy[j], (0, 1))
+            gate_product(nc.gpsimd, u, dgate[j][:, 1])
+            half_sigmoid_products(v)
+            if j in BOTH_IN_PSUM:
+                gate_copy[v] = copy_to_psum(v, gate_tiles)
+                d_up_from_gate(u, gate_copy[u], dup[j][:, 0])
+            else:
+                d_up_from_d_h(u, dup[j][:, 0])
+            d_up_from_gate(v, gate_copy[v], dup[j][:, 1])
+
+            if more:
+                first_matmuls(u + 2)
+                first_matmuls(v + 2)
+                even_copies(j + 1)
+            parts = activations(j + 1) if more else []
+            for n in range(max(len(parts), len(pending))):
+                if n < len(pending):
+                    store(pending[n])
+                if n < len(parts):
+                    part, i = parts[n]
+                    part(i)
+
+            if j == 0:
                 quantize_x(0)
                 quantize_x(1)
-            if step == 2:
-                surprise_factor()
-            if 1 <= step <= UNITS:
-                quantize(step - 1)
-                second_matmuls(step - 1)
-            if step < UNITS:
-                up_products(step)
-            if step + 1 < UNITS:
-                copy_to_psum(step + 1)
-            if step == 1:
+            up_products(v, column_block(up_tiles, v), (0,) if more else (0, 1))
+            quantize([("up", u), ("up", v)], dup[j][:], "up")
+            if not more:
+                gate_product(nc.vector, v, dgate[j + 1][:, 0])
+            if j == 0:
                 total_of_squares()
-            if step < UNITS:
-                gate_product(step)
-            if step >= 2:
-                store(step - 2, 0)
-                store(step - 2, 1)
-            if step + 2 < UNITS:
-                tanh_part(step + 2)
-                silu_part(step + 2)
-                mirrored_part(step + 2)
+                quantize([("gate", u)], dgate[j][:, 1:2], "gate")
+                pending = [("up", u), ("up", v), ("gate", u)]
+            else:
+                quantize([("gate", u - 1), ("gate", u)], dgate[j][:], "gate")
+                pending = [("up", u), ("up", v), ("gate", u - 1), ("gate", u)]
+            for n, key in enumerate(pending):
+                second_matmuls(key, not more and n >= 2)
+            if more:
+                up_products(v, column_block(up_tiles, v), (1,))
+                gate_product(nc.gpsimd, v, dgate[j + 1][:, 0])
+
+        quantize([("gate", UNITS - 1)], dgate[PAIRS][:, 0:1], "gate")
+        second_matmuls(("gate", UNITS - 1), True)
+        for key in pending:
+            store(key)
+        store(("gate", UNITS - 1), on_vector=True)

@@ -22,8 +22,8 @@ GROUP = P * PACK
 GROUPS = TOKENS // GROUP
 UNIT = 128
 UNITS = H // UNIT
-CHUNKS = (256, 256, 512, 512, 512)
-W_CHUNKS = (256, 768, 1024)
+CHUNKS = (256, 256, 256, 256, 512, 512)
+W_CHUNKS = (256, 256, 512, 1024)
 PAIRS = UNITS // 2
 BOTH_IN_PSUM = (0, 1, 2)
 
@@ -64,10 +64,13 @@ def tile_continuummemorysystem_pa_w8_kernel(
         ones = keep.tile([P, P], F32)
         planes = keep.tile([P, H], U8, align_bytes=64)
         silu_warm = keep.tile([P, 1], F32)
+        multiples = keep.tile([P, 3], F32)
         nc.vector.memset(one_col[:], 1.0)
         nc.vector.memset(planes[:].bitcast(I32), 0)
         nc.vector.memset(half[:], 0.5)
         nc.vector.memset(ones[:], 1.0)
+        for column, multiple in enumerate((1.0, 0.5, -0.5)):
+            nc.vector.memset(multiples[:, column : column + 1], multiple / TOKENS)
         nc.scalar.activation(out=silu_warm[:], in_=one_col[:], func=ACT.Silu)
         ident_f32 = keep.tile([P, P], F32)
         ident_bf = keep.tile([P, P], BF16)
@@ -91,6 +94,10 @@ def tile_continuummemorysystem_pa_w8_kernel(
             e = keep.tile([P, PACK, D], BF16, name=f"err_raw{g}")
             nc.sync.dma_start(out=e[:], in_=err_view[g])
             err_raw.append(e)
+
+        scale_rows = w_scales[0].rearrange("(q r) n -> r q n", r=4)
+        for r in range(4):
+            nc.sync.dma_start(out=planes[r:P:32, :].bitcast(I32), in_=scale_rows[r].bitcast(I32))
 
         w_flat = w_words[0].rearrange("p n t -> p (n t)")
         w_tiles = [keep.tile([P, w], U32, align_bytes=64, name=f"w{c}") for c, w in enumerate(W_CHUNKS)]
@@ -116,20 +123,12 @@ def tile_continuummemorysystem_pa_w8_kernel(
         load_x(1)
         load_h(gate_view, gate_tiles, 0)
         load_w(0)
-        for q in range(4):
-            nc.sync.dma_start(
-                out=planes[32 * q : 32 * q + 4, :].bitcast(I32),
-                in_=w_scales[0, 4 * q : 4 * q + 4, :].bitcast(I32),
-            )
         load_h(up_view, up_tiles, 0)
-        load_h(gate_view, gate_tiles, 1)
-        load_h(up_view, up_tiles, 1)
-        load_w(1)
-        for c in range(2, len(CHUNKS)):
+        for c in range(1, len(CHUNKS)):
             load_h(gate_view, gate_tiles, c)
+            if c < len(W_CHUNKS):
+                load_w(c)
             load_h(up_view, up_tiles, c)
-            if c == 2:
-                load_w(2)
 
         x_wide = keep.tile([P, GROUPS * PACK, D], BF16)
         x_grouped = keep.tile([P, GROUPS, D, PACK], BF16, align_bytes=64)
@@ -248,9 +247,11 @@ def tile_continuummemorysystem_pa_w8_kernel(
                 nc.tensor.matmul(bank[:, slots(g), :], ident_bf[:], source[:, slots(g), :], start=True, stop=True)
             return bank
 
-        def half_sigmoid_products(i):
+        def half_sigmoid_products(i, between=None):
             p2[i] = work.tile([P, GROUPS, UNIT, PACK], F32, name="p2")
             for g in range(GROUPS):
+                if between is not None:
+                    between(g)
                 nc.vector.scalar_tensor_tensor(
                     out=p2[i][:, g],
                     in0=th[i][:, g],
@@ -260,10 +261,12 @@ def tile_continuummemorysystem_pa_w8_kernel(
                     op1=ALU.mult,
                 )
 
-        def up_products(i, up, groups):
+        def up_products(i, up, groups, between=None):
             if 0 in groups:
                 yy[i] = work.tile([P, GROUPS, UNIT, PACK], F32, name="yy")
             for g in groups:
+                if between is not None:
+                    between(2 + g)
                 nc.vector.scalar_tensor_tensor(
                     out=yy[i][:, g],
                     in0=sl[i][:, g],
@@ -351,20 +354,15 @@ def tile_continuummemorysystem_pa_w8_kernel(
             nc.vector.tensor_scalar(out=mean2[:], in0=bank[:, 0:1], scalar1=1.0 / (TOKENS * TOKENS), scalar2=None, op0=ALU.mult)
             nc.gpsimd.tensor_tensor(out=mag[:], in0=mean2[:], in1=half[:], op=ALU.pow)
 
-        def surprise_factor():
-            nc.vector.tensor_scalar(out=ema[:], in0=mag[:], scalar1=0.05, scalar2=0.95, op0=ALU.mult, op1=ALU.add)
-            nc.vector.tensor_scalar(out=ema[:], in0=ema[:], scalar1=1e-8, scalar2=None, op0=ALU.max)
-            nc.vector.reciprocal(out=inv[:], in_=ema[:])
-            nc.vector.tensor_tensor(out=ratio[:], in0=mag[:], in1=inv[:], op=ALU.mult)
-            for column, multiple in enumerate((1.0, 0.5, -0.5)):
-                nc.vector.tensor_scalar(
-                    out=factor[:, column : column + 1],
-                    in0=ratio[:],
-                    scalar1=3.0,
-                    scalar2=multiple / TOKENS,
-                    op0=ALU.min,
-                    op1=ALU.mult,
-                )
+        def surprise_step(n):
+            if n == 0:
+                nc.vector.tensor_scalar(out=ema[:], in0=mag[:], scalar1=0.05, scalar2=0.95, op0=ALU.mult, op1=ALU.add)
+            elif n == 1:
+                nc.vector.reciprocal(out=inv[:], in_=ema[:])
+            elif n == 2:
+                nc.vector.tensor_scalar(out=ratio[:], in0=inv[:], scalar1=mag[:], scalar2=3.0, op0=ALU.mult, op1=ALU.min)
+            else:
+                nc.vector.tensor_scalar(out=factor[:], in0=multiples[:], scalar1=ratio[:], scalar2=None, op0=ALU.mult)
 
         def even_copies(j):
             up_copy[j] = copy_to_psum(2 * j, up_tiles)
@@ -397,10 +395,9 @@ def tile_continuummemorysystem_pa_w8_kernel(
             dgate[j + 1] = pair_tile("dgate")
             dup[j] = pair_tile("dup")
 
-            half_sigmoid_products(u)
-            if j == 1:
-                surprise_factor()
-            up_products(u, up_copy[j], (0, 1))
+            between = surprise_step if j == 1 else None
+            half_sigmoid_products(u, between)
+            up_products(u, up_copy[j], (0, 1), between)
             gate_product(nc.gpsimd, u, dgate[j][:, 1])
             half_sigmoid_products(v)
             if j in BOTH_IN_PSUM:

from contextlib import ExitStack

import concourse.mybir as mybir
from concourse.masks import make_identity

TOKENS, D, H = 1024, 512, 2048
FLOPS = 3 * 2 * TOKENS * D * H

F32 = mybir.dt.float32
BF16 = mybir.dt.bfloat16
I32 = mybir.dt.int32
U32 = mybir.dt.uint32
U8 = mybir.dt.uint8
FP8 = mybir.dt.float8_e4m3fn
FP8X4 = mybir.dt.float8_e4m3fn_x4
ALU = mybir.AluOpType
ACT = mybir.ActivationFunctionType

P = 128
PACK = 4
GROUP = P * PACK
GROUPS = TOKENS // GROUP
UNIT = 128
UNITS = H // UNIT
CHUNKS = (256, 256, 256, 256, 512, 512)
W_CHUNKS = (256, 256, 512, 1024)
PAIRS = UNITS // 2
BOTH_IN_PSUM = (0, 1, 2)


def starts_of(widths):
    starts = []
    for w in widths:
        starts.append(sum(widths[: len(starts)]))
    return starts


def locate(starts, widths, h0):
    for c, (s, w) in enumerate(zip(starts, widths)):
        if s <= h0 < s + w:
            return c, h0 - s
    raise ValueError("h0 out of range")


def tile_continuummemorysystem_pa_w8_kernel(
    tc, err, w_words, w_scales, gate_pre, up_pre, x_bytes, x_scale, out_0, out_1
):
    nc = tc.nc
    chunk_starts = starts_of(CHUNKS)
    w_starts = starts_of(W_CHUNKS)

    with ExitStack() as ctx:
        keep = ctx.enter_context(tc.tile_pool(name="keep", bufs=1))
        acts = ctx.enter_context(tc.tile_pool(name="acts", bufs=4))
        work = ctx.enter_context(tc.tile_pool(name="work", bufs=3))
        results = ctx.enter_context(tc.tile_pool(name="results", bufs=4))
        dh_pool = ctx.enter_context(tc.psum_pool(name="dh_pool", bufs=4))
        copy_pool = ctx.enter_context(tc.psum_pool(name="copy_pool", bufs=2))
        out_pool = ctx.enter_context(tc.psum_pool(name="out_pool", bufs=2))
        ctx.enter_context(tc.manual_schedule())

        one_col = keep.tile([P, 1], F32)
        half = keep.tile([P, 1], F32)
        ones = keep.tile([P, P], F32)
        planes = keep.tile([P, H], U8, align_bytes=64)
        silu_warm = keep.tile([P, 1], F32)
        multiples = keep.tile([P, 3], F32)
        nc.vector.memset(one_col[:], 1.0)
        nc.vector.memset(planes[:].bitcast(I32), 0)
        nc.vector.memset(half[:], 0.5)
        nc.vector.memset(ones[:], 1.0)
        for column, multiple in enumerate((1.0, 0.5, -0.5)):
            nc.vector.memset(multiples[:, column : column + 1], multiple / TOKENS)
        nc.scalar.activation(out=silu_warm[:], in_=one_col[:], func=ACT.Silu)
        ident_f32 = keep.tile([P, P], F32)
        ident_bf = keep.tile([P, P], BF16)
        make_identity(nc, ident_f32[:])
        make_identity(nc, ident_bf[:])

        x_raw = keep.tile([P, GROUPS * PACK, D], U8, align_bytes=64)
        xs = keep.tile([P, GROUPS * PACK], F32)
        x_view = x_bytes.rearrange("(g p t) n -> g p t n", p=P, t=PACK)
        def load_x(g):
            nc.sync.dma_start(out=x_raw[:, PACK * g : PACK * (g + 1), :], in_=x_view[g])

        load_x(0)
        nc.sync.dma_start(
            out=xs[:].rearrange("p (g t) -> p g t", t=PACK), in_=x_scale.rearrange("(g p t) o -> p g (t o)", p=P, t=PACK)
        )

        err_view = err.rearrange("(g p t) k -> g p t k", p=P, t=PACK)
        err_raw = []
        for g in range(GROUPS):
            e = keep.tile([P, PACK, D], BF16, name=f"err_raw{g}")
            nc.sync.dma_start(out=e[:], in_=err_view[g])
            err_raw.append(e)

        scale_rows = w_scales[0].rearrange("(q r) n -> r q n", r=4)
        for r in range(4):
            nc.sync.dma_start(out=planes[r:P:32, :].bitcast(I32), in_=scale_rows[r].bitcast(I32))

        w_flat = w_words[0].rearrange("p n t -> p (n t)")
        w_tiles = [keep.tile([P, w], U32, align_bytes=64, name=f"w{c}") for c, w in enumerate(W_CHUNKS)]

        def load_w(c):
            a, w = w_starts[c], W_CHUNKS[c]
            nc.sync.dma_start(
                out=w_tiles[c][:].bitcast(I32), in_=w_flat[:, PACK * a : PACK * (a + w)].bitcast(I32)
            )

        gate_view = gate_pre.rearrange("(g p t) h -> g p t h", p=P, t=PACK)
        up_view = up_pre.rearrange("(g p t) h -> g p t h", p=P, t=PACK)
        gate_tiles = [keep.tile([P, GROUPS * PACK, w], BF16, name=f"gate{c}") for c, w in enumerate(CHUNKS)]
        up_tiles = [keep.tile([P, GROUPS * PACK, w], BF16, name=f"up{c}") for c, w in enumerate(CHUNKS)]

        def load_h(view, tiles, c):
            a, w = chunk_starts[c], CHUNKS[c]
            for g in range(GROUPS):
                nc.sync.dma_start(
                    out=tiles[c][:, PACK * g : PACK * (g + 1), :], in_=view[g][:, :, a : a + w]
                )

        load_x(1)
        load_h(gate_view, gate_tiles, 0)
        load_w(0)
        load_h(up_view, up_tiles, 0)
        for c in range(1, len(CHUNKS)):
            load_h(gate_view, gate_tiles, c)
            if c < len(W_CHUNKS):
                load_w(c)
            load_h(up_view, up_tiles, c)

        x_wide = keep.tile([P, GROUPS * PACK, D], BF16)
        x_grouped = keep.tile([P, GROUPS, D, PACK], BF16, align_bytes=64)
        x_codes = keep.tile([P, GROUPS, D], U32, align_bytes=64)
        x_scales = keep.tile([P, GROUPS, D], U8, align_bytes=64)

        def widen_x(g):
            for j in range(PACK * g, PACK * (g + 1)):
                nc.vector.tensor_scalar(
                    out=x_wide[:, j, :], in0=x_raw[:, j, :].bitcast(FP8), scalar1=xs[:, j : j + 1], scalar2=None, op0=ALU.mult
                )
            if g == 0:
                nc.vector.tensor_copy(
                    out=x_grouped[:, g].rearrange("p (c i) t -> p c t i", i=4),
                    in_=x_wide[:, PACK * g : PACK * (g + 1), :].rearrange("p t (c i) -> p c t i", i=4),
                )
            for n in range(0, D if g == 1 else 0, P):
                nc.gpsimd.tensor_scalar(
                    out=x_grouped[:, g, n : n + P, :],
                    in0=x_wide[:, PACK * g : PACK * (g + 1), n : n + P].rearrange("p t n -> p n t"),
                    scalar1=1.0,
                    scalar2=0.0,
                    op0=ALU.mult,
                    op1=ALU.add,
                )

        def quantize_x(g):
            nc.vector.quantize_mx(
                out=x_codes[:, g, :].bitcast(FP8X4),
                scales=x_scales[:, g, :],
                in_=x_grouped[:, g].rearrange("p n t -> p (n t)"),
            )

        widen_x(0)

        err_grouped = [keep.tile([P, PACK, P, PACK], BF16, align_bytes=64, name=f"err_grouped{g}") for g in range(GROUPS)]
        sums = keep.tile([P, 3], F32)
        square_junk = keep.tile([P, PACK * D], BF16)

        def square_err(part, g, first, last):
            nc.scalar.activation(
                out=square_junk[:, : D * (last - first)],
                in_=err_raw[g][:, first:last, :].rearrange("p t k -> p (t k)"),
                func=ACT.Square,
                accum_out=sums[:, part : part + 1],
            )

        square_err(0, 0, 0, 2)
        err_codes = keep.tile([P, GROUPS, PACK * P], U32, align_bytes=64)
        err_scales = keep.tile([P, GROUPS, PACK * P], U8, align_bytes=64)
        for g in range(GROUPS):
            for pair in range(2):
                bank = out_pool.tile([P, 2, 2, P], F32, tag="out")
                for s in range(2):
                    words = err_raw[g][:, 2 * pair + s, :].bitcast(F32)
                    for u in range(2):
                        nc.tensor.transpose(bank[:, s, u, :], words[:, u : D // 2 : 2], ident_f32[:])
                nc.scalar.copy(
                    out=err_grouped[g][:, 2 * pair : 2 * pair + 2].rearrange("p s r e -> p s (r e)").bitcast(F32).rearrange(
                        "p s (r u) -> p s r u", u=2
                    ),
                    in_=bank[:].rearrange("p s u r -> p s r u"),
                )
            nc.vector.quantize_mx(
                out=err_codes[:, g, :].bitcast(FP8X4),
                scales=err_scales[:, g, :],
                in_=err_grouped[g][:].rearrange("p t r e -> p (t r e)"),
            )
            if g == 0:
                widen_x(1)

        th, si, sl, dh, copied, p2, yy, dup, dgate, codes, banks = {}, {}, {}, {}, {}, {}, {}, {}, {}, {}, {}

        def column_block(tiles, i):
            c, off = locate(chunk_starts, CHUNKS, UNIT * i)
            return tiles[c][:, :, off : off + UNIT]

        def slots(g):
            return slice(PACK * g, PACK * (g + 1))

        def activation_of_gate(i, name, func, scale):
            t = acts.tile([P, GROUPS, UNIT, PACK], F32, tag=name, name=name, bufs=2 if name == "si" else 4)
            view = column_block(gate_tiles, i).rearrange("p (g t) n -> p g n t", t=PACK)
            nc.scalar.activation(out=t[:], in_=view, func=func, scale=scale)
            return t

        def tanh_part(i):
            th[i] = activation_of_gate(i, "th", ACT.Tanh, 0.5)

        def mirrored_part(i):
            sl[i] = activation_of_gate(i, "sl", ACT.Silu, -1.0)

        def silu_part(i):
            si[i] = activation_of_gate(i, "si", ACT.Silu, 1.0)

        def first_matmuls(i):
            c, off = locate(w_starts, W_CHUNKS, UNIT * i)
            for g in range(GROUPS):
                bank = dh_pool.tile([P, PACK, UNIT], F32, tag="dh")
                for t in range(PACK):
                    nc.tensor.matmul_mx(
                        out=bank[:, t, :],
                        lhsT=err_codes[:, g, P * t : P * (t + 1)].bitcast(FP8X4),
                        lhsT_scale=err_scales[:, g, P * t : P * (t + 1)],
                        rhs=w_tiles[c][:, off : off + UNIT].bitcast(FP8X4),
                        rhs_scale=planes[:, UNIT * i : UNIT * (i + 1)],
                        start=True,
                        stop=True,
                    )
                dh[i, g] = bank

        def copy_to_psum(i, tiles):
            bank = copy_pool.tile([P, GROUPS * PACK, UNIT], BF16, tag="copied")
            source = column_block(tiles, i)
            for g in range(GROUPS):
                nc.tensor.matmul(bank[:, slots(g), :], ident_bf[:], source[:, slots(g), :], start=True, stop=True)
            return bank

        def half_sigmoid_products(i, between=None):
            p2[i] = work.tile([P, GROUPS, UNIT, PACK], F32, name="p2")
            for g in range(GROUPS):
                if between is not None:
                    between(g)
                nc.vector.scalar_tensor_tensor(
                    out=p2[i][:, g],
                    in0=th[i][:, g],
                    scalar=1.0,
                    in1=dh[i, g][:].rearrange("p t n -> p n t"),
                    op0=ALU.add,
                    op1=ALU.mult,
                )

        def up_products(i, up, groups, between=None):
            if 0 in groups:
                yy[i] = work.tile([P, GROUPS, UNIT, PACK], F32, name="yy")
            for g in groups:
                if between is not None:
                    between(2 + g)
                nc.vector.scalar_tensor_tensor(
                    out=yy[i][:, g],
                    in0=sl[i][:, g],
                    scalar=-1.0,
                    in1=up[:, slots(g), :].rearrange("p t n -> p n t"),
                    op0=ALU.add,
                    op1=ALU.mult,
                )

        def d_up_from_d_h(i, out):
            for g in range(GROUPS):
                nc.vector.tensor_tensor(
                    out=out[:, g], in0=dh[i, g][:].rearrange("p t n -> p n t"), in1=si[i][:, g], op=ALU.mult
                )

        def d_up_from_gate(i, gate, out):
            nc.vector.tensor_tensor(
                out=out, in0=p2[i][:], in1=gate[:].rearrange("p (g t) n -> p g n t", t=PACK), op=ALU.mult
            )

        def gate_product(engine, i, out):
            engine.tensor_tensor(
                out=out.rearrange("p g n t -> p (g n t)"),
                in0=p2[i][:].rearrange("p g n t -> p (g n t)"),
                in1=yy[i][:].rearrange("p g n t -> p (g n t)"),
                op=ALU.mult,
            )

        def pair_tile(name):
            return work.tile([P, 2, GROUPS, UNIT, PACK], BF16, tag=name, name=name, align_bytes=64, bufs=2)

        def quantize(keys, values, name):
            n = len(keys) * GROUPS * UNIT
            c = work.tile([P, 2 * GROUPS * UNIT], U32, tag=name + "_codes", name="codes_tile", align_bytes=64, bufs=3)
            s = work.tile([P, 2 * GROUPS * UNIT], U8, tag=name + "_scales", name="scales_tile", align_bytes=64, bufs=3)
            nc.vector.quantize_mx(
                out=c[:, :n].bitcast(FP8X4), scales=s[:, :n], in_=values.rearrange("p k g n t -> p (k g n t)")
            )
            for slot, key in enumerate(keys):
                codes[key] = (c, s, slot * GROUPS * UNIT)

        def second_matmuls(key, spare_bank):
            c, s, base = codes[key]
            if spare_bank:
                bank = dh_pool.tile([P, D], F32, tag="dh")
            else:
                bank = out_pool.tile([P, D], F32, tag="out")
            for g in range(GROUPS):
                a = base + UNIT * g
                nc.tensor.matmul_mx(
                    out=bank[:],
                    lhsT=c[:, a : a + UNIT].bitcast(FP8X4),
                    lhsT_scale=s[:, a : a + UNIT],
                    rhs=x_codes[:, g, :].bitcast(FP8X4),
                    rhs_scale=x_scales[:, g, :],
                    start=(g == 0),
                    stop=(g == GROUPS - 1),
                )
            banks[key] = bank

        def store(key, on_vector=False):
            kind, i = key
            res = results.tile([P, D], F32, tag="res", name="res", bufs=8)
            column = 2 if kind == "gate" else 1 if i % 2 == 1 or i // 2 in BOTH_IN_PSUM else 0
            if on_vector:
                nc.vector.tensor_scalar(
                    out=res[:], in0=banks[key][:], scalar1=factor[:, column : column + 1], scalar2=None, op0=ALU.mult
                )
            else:
                nc.scalar.activation(out=res[:], in_=banks[key][:], func=ACT.Copy, scale=factor[:, column : column + 1])
            out = out_1 if kind == "gate" else out_0
            nc.sync.dma_start(out=out[UNIT * i : UNIT * (i + 1), :], in_=res[:])

        mean2 = keep.tile([P, 1], F32)
        mag = keep.tile([P, 1], F32)
        ema = keep.tile([P, 1], F32)
        inv = keep.tile([P, 1], F32)
        ratio = keep.tile([P, 1], F32)
        factor = keep.tile([P, 3], F32)

        def total_of_squares():
            bank = out_pool.tile([P, D], F32, tag="out")
            for part in range(3):
                nc.tensor.matmul(bank[:, 0:1], ones[:], sums[:, part : part + 1], start=(part == 0), stop=(part == 2))
            nc.vector.tensor_scalar(out=mean2[:], in0=bank[:, 0:1], scalar1=1.0 / (TOKENS * TOKENS), scalar2=None, op0=ALU.mult)
            nc.gpsimd.tensor_tensor(out=mag[:], in0=mean2[:], in1=half[:], op=ALU.pow)

        def surprise_step(n):
            if n == 0:
                nc.vector.tensor_scalar(out=ema[:], in0=mag[:], scalar1=0.05, scalar2=0.95, op0=ALU.mult, op1=ALU.add)
            elif n == 1:
                nc.vector.reciprocal(out=inv[:], in_=ema[:])
            elif n == 2:
                nc.vector.tensor_scalar(out=ratio[:], in0=inv[:], scalar1=mag[:], scalar2=3.0, op0=ALU.mult, op1=ALU.min)
            else:
                nc.vector.tensor_scalar(out=factor[:], in0=multiples[:], scalar1=ratio[:], scalar2=None, op0=ALU.mult)

        def even_copies(j):
            up_copy[j] = copy_to_psum(2 * j, up_tiles)
            if j in BOTH_IN_PSUM:
                gate_copy[2 * j] = copy_to_psum(2 * j, gate_tiles)
            else:
                gate_copy[2 * j + 1] = copy_to_psum(2 * j + 1, gate_tiles)

        def activations(j):
            u, v = 2 * j, 2 * j + 1
            parts = [(tanh_part, u), (mirrored_part, u), (tanh_part, v), (mirrored_part, v)]
            if j not in BOTH_IN_PSUM:
                parts = parts[:2] + [(silu_part, u)] + parts[2:]
            return parts

        up_copy, gate_copy = {}, {}
        for part, i in activations(0):
            part(i)
        square_err(1, 0, 2, 4)
        square_err(2, 1, 0, 4)
        first_matmuls(0)
        even_copies(0)
        first_matmuls(1)

        pending = []
        dgate[0] = pair_tile("dgate")
        for j in range(PAIRS):
            u, v = 2 * j, 2 * j + 1
            more = j + 1 < PAIRS
            dgate[j + 1] = pair_tile("dgate")
            dup[j] = pair_tile("dup")

            between = surprise_step if j == 1 else None
            half_sigmoid_products(u, between)
            up_products(u, up_copy[j], (0, 1), between)
            gate_product(nc.gpsimd, u, dgate[j][:, 1])
            half_sigmoid_products(v)
            if j in BOTH_IN_PSUM:
                gate_copy[v] = copy_to_psum(v, gate_tiles)
                d_up_from_gate(u, gate_copy[u], dup[j][:, 0])
            else:
                d_up_from_d_h(u, dup[j][:, 0])
            d_up_from_gate(v, gate_copy[v], dup[j][:, 1])

            if more:
                first_matmuls(u + 2)
                first_matmuls(v + 2)
                even_copies(j + 1)
            parts = activations(j + 1) if more else []
            for n in range(max(len(parts), len(pending))):
                if n < len(pending):
                    store(pending[n])
                if n < len(parts):
                    part, i = parts[n]
                    part(i)

            if j == 0:
                quantize_x(0)
                quantize_x(1)
            up_products(v, column_block(up_tiles, v), (0,) if more else (0, 1))
            quantize([("up", u), ("up", v)], dup[j][:], "up")
            if not more:
                gate_product(nc.vector, v, dgate[j + 1][:, 0])
            if j == 0:
                total_of_squares()
                quantize([("gate", u)], dgate[j][:, 1:2], "gate")
                pending = [("up", u), ("up", v), ("gate", u)]
            else:
                quantize([("gate", u - 1), ("gate", u)], dgate[j][:], "gate")
                pending = [("up", u), ("up", v), ("gate", u - 1), ("gate", u)]
            for n, key in enumerate(pending):
                second_matmuls(key, not more and n >= 2)
            if more:
                up_products(v, column_block(up_tiles, v), (1,))
                gate_product(nc.gpsimd, v, dgate[j + 1][:, 0])

        quantize([("gate", UNITS - 1)], dgate[PAIRS][:, 0:1], "gate")
        second_matmuls(("gate", UNITS - 1), True)
        for key in pending:
            store(key)
        store(("gate", UNITS - 1), on_vector=True)
